import numpy as np
import ml_dtypes


def mxq(x, axis, fmt="e4m3"):
    dtype, down = {"e4m3": (ml_dtypes.float8_e4m3fn, 7), "e5m2": (ml_dtypes.float8_e5m2, 14)}[fmt]
    v = np.moveaxis(np.asarray(x, np.float32).astype(ml_dtypes.bfloat16).astype(np.float64), axis, -1)
    blocks = v.reshape(v.shape[:-1] + (-1, 32))
    amax = np.abs(blocks).max(-1, keepdims=True)
    byte = np.maximum(np.where(amax > 0, np.frexp(amax)[1] - 1 + 127, 0) - down, 1)
    scale = np.exp2(byte - 127.0)
    codes = (blocks / scale).astype(np.float32).astype(dtype).astype(np.float64)
    return np.moveaxis((codes * scale).reshape(v.shape), -1, axis)


WIDE = False


def mx_kscale(k):
    if not WIDE:
        return np.ones(k)
    levels = np.array([10, -10, 5, -5, 0])
    a = np.random.permutation(np.resize(levels, k // 512 * 4)).reshape(k // 512, 4)
    idx = np.arange(k)
    return np.exp2(a[idx // 512, idx % 128 // 32])


BF16 = ml_dtypes.bfloat16


def bf(x):
    return np.asarray(x, np.float32).astype(BF16)


def f64(x):
    return np.asarray(x).astype(np.float64)


E2M1 = np.array([0.0, 0.5, 1.0, 1.5, 2.0, 3.0, 4.0, 6.0, -0.0, -0.5, -1.0, -1.5, -2.0, -3.0, -4.0, -6.0])


def pack_weight(w, fmt):
    k, n = w.shape
    w = f64(bf(w)).reshape(k // 32, 32, n)
    amax = np.abs(w).max(1)
    if fmt == "e4m3":
        byte = np.frexp(amax)[1] - 1 + 127 - 7
    else:
        mant, ex = np.frexp(amax / 6.0)
        byte = np.where(mant > 0.5, ex, ex - 1) + 127
    byte = np.clip(np.where(amax > 0, byte, 1), 1, 254)
    scaled = (w * np.exp2(127.0 - byte)[:, None, :]).reshape(k, n).astype(np.float32)
    by_word = np.ascontiguousarray(scaled.reshape(k // 512, 128, 4, n).transpose(0, 1, 3, 2))
    if fmt == "e4m3":
        words = by_word.astype(ml_dtypes.float8_e4m3fn).view(np.uint8)
    else:
        c = by_word.astype(ml_dtypes.float4_e2m1fn).view(np.uint8) & 0xF
        words = c[..., 0::2] | (c[..., 1::2] << 4)
    return np.ascontiguousarray(words), np.ascontiguousarray(byte.astype(np.uint8).reshape(k // 512, 16, n))


def unpack_weight(words, scales, fmt):
    g, p, n, _ = words.shape
    if fmt == "e4m3":
        vals = np.ascontiguousarray(words).view(ml_dtypes.float8_e4m3fn).astype(np.float64)
    else:
        nib = np.empty((g, p, n, 4), np.uint8)
        nib[..., 0::2] = words & 0xF
        nib[..., 1::2] = words >> 4
        vals = E2M1[nib]
    vals = vals * np.repeat(np.exp2(scales.astype(np.float64) - 127.0), 8, axis=1)[..., None]
    return vals.transpose(0, 1, 3, 2).reshape(g * 512, n)

def pack4(w):
    words, scales = pack_weight(w, "e2m1")
    return words.reshape(words.shape[0], 128, -1), scales


def unpack4(words, scales):
    return unpack_weight(words.reshape(words.shape[0], 128, -1, 2), scales, "e2m1")


N, H, S, R, T = 16384, 512, 4, 128, 128


def setup_inputs():
    s = mx_kscale(H)
    encodings = bf(np.random.standard_normal((N, H)) * s)
    domain_encs = bf(np.random.standard_normal((S, H)) * s)
    stack = np.random.standard_normal((S, H, R)) / np.sqrt(H) / s[None, :, None]
    words, scales = pack4(stack.reshape(-1, R))
    return {"encodings": encodings,
            "domain_encs": domain_encs,
            "Us_words": words,
            "Us_scales": scales}


def reference(encodings, domain_encs, Us_words, Us_scales):
    diff = f64(encodings)[None, :, :] - f64(domain_encs)[:, None, :]
    proj = mxq(diff, 2, "e4m3") @ unpack4(Us_words, Us_scales).reshape(S, H, R)
    dist = np.sqrt(np.sum(proj * proj, axis=-1))
    z = -dist
    e = np.exp(z - z.max(axis=0, keepdims=True))
    return e / e.sum(axis=0, keepdims=True)

@@ -1,0 +1,183 @@
+from contextlib import ExitStack
+
+import concourse.mybir as mybir
+from concourse.masks import make_identity
+
+F32 = mybir.dt.float32
+BF16 = mybir.dt.bfloat16
+I32 = mybir.dt.int32
+U32 = mybir.dt.uint32
+U8 = mybir.dt.uint8
+FP8X4 = mybir.dt.float8_e4m3fn_x4
+FP4X4 = mybir.dt.float4_e2m1fn_x4
+ALU = mybir.AluOpType
+ACT = mybir.ActivationFunctionType
+AXIS_X = mybir.AxisListType.X
+
+P = 128
+PACK = 4
+TOKENS, HIDDEN, SOURCES, RANK = 16384, 512, 4, 128
+assert HIDDEN == P * PACK
+
+TILES = TOKENS // P
+GROUP_TILES = 2
+GROUP = GROUP_TILES * P
+GROUPS = TILES // GROUP_TILES
+HALVES = 2
+WORDS = HIDDEN // 2
+
+LOAD_AHEAD = 6
+TRANSPOSE_AHEAD = 2
+
+SQRT_FLOOR = 2.0 ** -116
+
+FLOPS = 2 * SOURCES * TOKENS * HIDDEN * RANK
+
+
+def tile_moe_pa_t_e_kernel(tc, encodings, domain_encs, Us_words, Us_scales, out):
+    nc = tc.nc
+    enc_rows = encodings.rearrange("(i j) k -> i j k", j=TILES)
+    out_cols = out.rearrange("s (i j) -> i s j", j=TILES)
+
+    with ExitStack() as ctx:
+        ctx.enter_context(tc.manual_schedule())
+        const = ctx.enter_context(tc.tile_pool(name="const", bufs=1))
+        enc_pool = ctx.enter_context(tc.tile_pool(name="enc", bufs=LOAD_AHEAD))
+        diff_pool = ctx.enter_context(tc.tile_pool(name="diff", bufs=2))
+        code_pool = ctx.enter_context(tc.tile_pool(name="code", bufs=3))
+        square_pool = ctx.enter_context(tc.tile_pool(name="square", bufs=2))
+        turned_pool = ctx.enter_context(tc.psum_pool(name="turned", bufs=TRANSPOSE_AHEAD + 1))
+        proj_pool = ctx.enter_context(tc.psum_pool(name="proj", bufs=2 * GROUP_TILES))
+
+        enc_of, turned_of, diff_of, codes_of, scales_of = {}, {}, {}, {}, {}
+
+        def load(g):
+            enc_sb = enc_pool.tile([P, GROUP_TILES, HIDDEN], BF16)
+            first = g * GROUP_TILES
+            nc.sync.dma_start(out=enc_sb[:], in_=enc_rows[:, first : first + GROUP_TILES, :])
+            enc_of[g] = enc_sb
+
+        def transpose(g):
+            turned = turned_pool.tile([P, HALVES, GROUP], F32)
+            for h in range(GROUP_TILES):
+                words = enc_of[g][:, h, :].bitcast(F32)
+                for u in range(HALVES):
+                    nc.tensor.transpose(
+                        turned[:, u, h * P : (h + 1) * P], words[:, u:WORDS:HALVES], identity[:]
+                    )
+            turned_of[g] = turned
+
+        def subtract(g):
+            diff = diff_pool.tile([P, SOURCES, GROUP, PACK], BF16, align_bytes=64)
+            pairs = turned_of[g][:].bitcast(BF16).rearrange("p u (n e) -> p n u e", e=2)
+            for s in range(SOURCES):
+                centre = dom_t[:, s, :].rearrange("p (u e) -> p u e", e=2).unsqueeze(1)
+                nc.vector.tensor_tensor(
+                    out=diff[:, s, :, :].rearrange("p n (u e) -> p n u e", e=2),
+                    in0=pairs,
+                    in1=centre.to_broadcast([P, GROUP, HALVES, 2]),
+                    op=ALU.subtract,
+                )
+            diff_of[g] = diff
+
+        def quantise(g):
+            codes = code_pool.tile([P, SOURCES, GROUP], U32, align_bytes=64)
+            scales = code_pool.tile([P, SOURCES, GROUP], U8, align_bytes=64)
+            nc.vector.quantize_mx(
+                out=codes[:].rearrange("p s n -> p (s n)").bitcast(FP8X4),
+                scales=scales[:].rearrange("p s n -> p (s n)"),
+                in_=diff_of[g][:].rearrange("p s n t -> p (s n t)"),
+            )
+            codes_of[g], scales_of[g] = codes, scales
+
+        def project(g):
+            squares = square_pool.tile([P, GROUP_TILES, SOURCES, RANK], F32)
+            for h in range(GROUP_TILES):
+                proj = proj_pool.tile([P, SOURCES, RANK], F32)
+                tokens = slice(h * P, (h + 1) * P)
+                for s in range(SOURCES):
+                    nc.tensor.matmul_mx(
+                        out=proj[:, s, :],
+                        lhsT=codes_of[g][:, s, tokens].bitcast(FP8X4),
+                        lhsT_scale=scales_of[g][:, s, tokens],
+                        rhs=u_words[:, s, :].bitcast(FP4X4),
+                        rhs_scale=u_scales[:, s, :],
+                        start=True,
+                        stop=True,
+                    )
+                j = g * GROUP_TILES + h
+                for s in range(SOURCES):
+                    nc.scalar.activation(
+                        out=squares[:, h, s, :],
+                        in_=proj[:, s, :],
+                        func=ACT.Square,
+                        accum_out=dist_sq[:, s, j : j + 1],
+                    )
+
+        dom_t = const.tile([P, SOURCES, PACK], BF16)
+        nc.sync.dma_start(out=dom_t[:], in_=domain_encs.rearrange("s (p t) -> p s t", t=PACK))
+        for g in range(TRANSPOSE_AHEAD):
+            load(g)
+        u_words = const.tile([P, SOURCES, 2 * RANK], U8, align_bytes=64)
+        nc.sync.dma_start(
+            out=u_words[:].bitcast(I32), in_=Us_words.rearrange("s p b -> p s b").bitcast(I32)
+        )
+        u_scales = const.tile([P, SOURCES, RANK], U8, align_bytes=64)
+        nc.vector.memset(u_scales[:].bitcast(I32), 0)
+        for quadrant in range(4):
+            nc.sync.dma_start(
+                out=u_scales[32 * quadrant : 32 * quadrant + 4].bitcast(I32),
+                in_=Us_scales[:, 4 * quadrant : 4 * quadrant + 4, :]
+                .rearrange("s r n -> r s n")
+                .bitcast(I32),
+            )
+        for g in range(TRANSPOSE_AHEAD, LOAD_AHEAD):
+            load(g)
+        identity = const.tile([P, P], F32)
+        make_identity(nc, identity[:])
+        warm = const.tile([P, 1], F32)
+        nc.vector.memset(warm[:], 1.0)
+        nc.scalar.activation(out=warm[:], in_=warm[:], func=ACT.Sqrt)
+        dist_sq = const.tile([P, SOURCES, TILES], F32)
+
+        for g in range(TRANSPOSE_AHEAD):
+            transpose(g)
+        for step in range(GROUPS + 2):
+            if step + LOAD_AHEAD < GROUPS:
+                load(step + LOAD_AHEAD)
+            if step >= 2:
+                project(step - 2)
+            if step + TRANSPOSE_AHEAD < GROUPS:
+                transpose(step + TRANSPOSE_AHEAD)
+            if step < GROUPS:
+                subtract(step)
+            if 1 <= step <= GROUPS:
+                quantise(step - 1)
+
+        dist = const.tile([P, SOURCES, TILES], F32)
+        nearest = const.tile([P, TILES], F32)
+        weight = const.tile([P, SOURCES, TILES], F32)
+        total = const.tile([P, TILES], F32)
+        nc.vector.tensor_scalar_max(out=dist_sq[:], in0=dist_sq[:], scalar1=SQRT_FLOOR)
+        nc.scalar.activation(out=dist[:], in_=dist_sq[:], func=ACT.Sqrt)
+        nc.vector.tensor_reduce(
+            out=nearest[:], in_=dist[:].rearrange("p s j -> p j s"), axis=AXIS_X, op=ALU.min
+        )
+        nc.vector.tensor_tensor(
+            out=dist[:],
+            in0=dist[:],
+            in1=nearest[:].unsqueeze(1).to_broadcast([P, SOURCES, TILES]),
+            op=ALU.subtract,
+        )
+        nc.scalar.activation(out=weight[:], in_=dist[:], func=ACT.Exp, scale=-1.0)
+        nc.vector.tensor_reduce(
+            out=total[:], in_=weight[:].rearrange("p s j -> p j s"), axis=AXIS_X, op=ALU.add
+        )
+        nc.vector.reciprocal(out=total[:], in_=total[:])
+        nc.vector.tensor_tensor(
+            out=weight[:],
+            in0=weight[:],
+            in1=total[:].unsqueeze(1).to_broadcast([P, SOURCES, TILES]),
+            op=ALU.mult,
+        )
+        nc.sync.dma_start(out=out_cols, in_=weight[:])

@@ -26,8 +26,13 @@ GROUPS = TILES // GROUP_TILES
 HALVES = 2
 WORDS = HIDDEN // 2
 
-LOAD_AHEAD = 6
-TRANSPOSE_AHEAD = 2
+BLOCK_GROUPS = SOURCES
+
+LOAD_AT = 0
+TURN_AT = 4
+SUBTRACT_AT = TURN_AT + BLOCK_GROUPS + 1
+QUANTISE_AT = SUBTRACT_AT + BLOCK_GROUPS
+PROJECT_AT = QUANTISE_AT + 1
 
 SQRT_FLOOR = 2.0 ** -116
 
@@ -42,11 +47,12 @@ def tile_moe_pa_t_e_kernel(tc, encodings, domain_encs, Us_words, Us_scales, out)
     with ExitStack() as ctx:
         ctx.enter_context(tc.manual_schedule())
         const = ctx.enter_context(tc.tile_pool(name="const", bufs=1))
-        enc_pool = ctx.enter_context(tc.tile_pool(name="enc", bufs=LOAD_AHEAD))
+        enc_pool = ctx.enter_context(tc.tile_pool(name="enc", bufs=TURN_AT + 2))
+        turned_pool = ctx.enter_context(tc.tile_pool(name="turned", bufs=3))
         diff_pool = ctx.enter_context(tc.tile_pool(name="diff", bufs=2))
         code_pool = ctx.enter_context(tc.tile_pool(name="code", bufs=3))
         square_pool = ctx.enter_context(tc.tile_pool(name="square", bufs=2))
-        turned_pool = ctx.enter_context(tc.psum_pool(name="turned", bufs=TRANSPOSE_AHEAD + 1))
+        plane_pool = ctx.enter_context(tc.psum_pool(name="plane", bufs=3))
         proj_pool = ctx.enter_context(tc.psum_pool(name="proj", bufs=2 * GROUP_TILES))
 
         enc_of, turned_of, diff_of, codes_of, scales_of = {}, {}, {}, {}, {}
@@ -57,36 +63,49 @@ def tile_moe_pa_t_e_kernel(tc, encodings, domain_encs, Us_words, Us_scales, out)
             nc.sync.dma_start(out=enc_sb[:], in_=enc_rows[:, first : first + GROUP_TILES, :])
             enc_of[g] = enc_sb
 
-        def transpose(g):
-            turned = turned_pool.tile([P, HALVES, GROUP], F32)
+        def turn(g):
+            planes = plane_pool.tile([P, HALVES, GROUP], F32)
             for h in range(GROUP_TILES):
                 words = enc_of[g][:, h, :].bitcast(F32)
                 for u in range(HALVES):
                     nc.tensor.transpose(
-                        turned[:, u, h * P : (h + 1) * P], words[:, u:WORDS:HALVES], identity[:]
+                        planes[:, u, h * P : (h + 1) * P], words[:, u:WORDS:HALVES], identity[:]
                     )
-            turned_of[g] = turned
+            b, c = divmod(g, BLOCK_GROUPS)
+            if c == 0:
+                turned = turned_pool.tile([P, BLOCK_GROUPS, GROUP, PACK], BF16)
+                turned_of[b] = turned
+            nc.scalar.copy(
+                out=turned_of[b][:, c, :, :]
+                .rearrange("p n t -> p (n t)")
+                .bitcast(F32)
+                .rearrange("p (n u) -> p n u", u=HALVES),
+                in_=planes[:].rearrange("p u n -> p n u"),
+            )
 
         def subtract(g):
-            diff = diff_pool.tile([P, SOURCES, GROUP, PACK], BF16, align_bytes=64)
-            pairs = turned_of[g][:].bitcast(BF16).rearrange("p u (n e) -> p n u e", e=2)
-            for s in range(SOURCES):
-                centre = dom_t[:, s, :].rearrange("p (u e) -> p u e", e=2).unsqueeze(1)
-                nc.vector.tensor_tensor(
-                    out=diff[:, s, :, :].rearrange("p n (u e) -> p n u e", e=2),
-                    in0=pairs,
-                    in1=centre.to_broadcast([P, GROUP, HALVES, 2]),
-                    op=ALU.subtract,
-                )
-            diff_of[g] = diff
+            b, s = divmod(g, SOURCES)
+            if s == 0:
+                diff = diff_pool.tile([P, BLOCK_GROUPS, SOURCES, GROUP, PACK], BF16, align_bytes=64)
+                diff_of[b] = diff
+            nc.vector.tensor_tensor(
+                out=diff_of[b][:, :, s, :, :],
+                in0=turned_of[b][:],
+                in1=dom_t[:, s, :]
+                .unsqueeze(1)
+                .unsqueeze(1)
+                .to_broadcast([P, BLOCK_GROUPS, GROUP, PACK]),
+                op=ALU.subtract,
+            )
 
         def quantise(g):
+            b, c = divmod(g, BLOCK_GROUPS)
             codes = code_pool.tile([P, SOURCES, GROUP], U32, align_bytes=64)
             scales = code_pool.tile([P, SOURCES, GROUP], U8, align_bytes=64)
             nc.vector.quantize_mx(
                 out=codes[:].rearrange("p s n -> p (s n)").bitcast(FP8X4),
                 scales=scales[:].rearrange("p s n -> p (s n)"),
-                in_=diff_of[g][:].rearrange("p s n t -> p (s n t)"),
+                in_=diff_of[b][:, c, :, :, :].rearrange("p s n t -> p (s n t)"),
             )
             codes_of[g], scales_of[g] = codes, scales
 
@@ -116,43 +135,40 @@ def tile_moe_pa_t_e_kernel(tc, encodings, domain_encs, Us_words, Us_scales, out)
 
         dom_t = const.tile([P, SOURCES, PACK], BF16)
         nc.sync.dma_start(out=dom_t[:], in_=domain_encs.rearrange("s (p t) -> p s t", t=PACK))
-        for g in range(TRANSPOSE_AHEAD):
-            load(g)
-        u_words = const.tile([P, SOURCES, 2 * RANK], U8, align_bytes=64)
-        nc.sync.dma_start(
-            out=u_words[:].bitcast(I32), in_=Us_words.rearrange("s p b -> p s b").bitcast(I32)
-        )
-        u_scales = const.tile([P, SOURCES, RANK], U8, align_bytes=64)
-        nc.vector.memset(u_scales[:].bitcast(I32), 0)
-        for quadrant in range(4):
-            nc.sync.dma_start(
-                out=u_scales[32 * quadrant : 32 * quadrant + 4].bitcast(I32),
-                in_=Us_scales[:, 4 * quadrant : 4 * quadrant + 4, :]
-                .rearrange("s r n -> r s n")
-                .bitcast(I32),
-            )
-        for g in range(TRANSPOSE_AHEAD, LOAD_AHEAD):
-            load(g)
         identity = const.tile([P, P], F32)
         make_identity(nc, identity[:])
         warm = const.tile([P, 1], F32)
         nc.vector.memset(warm[:], 1.0)
         nc.scalar.activation(out=warm[:], in_=warm[:], func=ACT.Sqrt)
         dist_sq = const.tile([P, SOURCES, TILES], F32)
+        u_words = const.tile([P, SOURCES, 2 * RANK], U8, align_bytes=64)
+        u_scales = const.tile([P, SOURCES, RANK], U8, align_bytes=64)
+        nc.vector.memset(u_scales[:].bitcast(I32), 0)
 
-        for g in range(TRANSPOSE_AHEAD):
-            transpose(g)
-        for step in range(GROUPS + 2):
-            if step + LOAD_AHEAD < GROUPS:
-                load(step + LOAD_AHEAD)
-            if step >= 2:
-                project(step - 2)
-            if step + TRANSPOSE_AHEAD < GROUPS:
-                transpose(step + TRANSPOSE_AHEAD)
-            if step < GROUPS:
-                subtract(step)
-            if 1 <= step <= GROUPS:
-                quantise(step - 1)
+        def load_weights():
+            nc.sync.dma_start(
+                out=u_words[:].bitcast(I32), in_=Us_words.rearrange("s p b -> p s b").bitcast(I32)
+            )
+            for quadrant in range(4):
+                nc.sync.dma_start(
+                    out=u_scales[32 * quadrant : 32 * quadrant + 4].bitcast(I32),
+                    in_=Us_scales[:, 4 * quadrant : 4 * quadrant + 4, :]
+                    .rearrange("s r n -> r s n")
+                    .bitcast(I32),
+                )
+
+        def at(stage, g):
+            if 0 <= g < GROUPS:
+                stage(g)
+
+        for tick in range(GROUPS + PROJECT_AT):
+            if tick == BLOCK_GROUPS:
+                load_weights()
+            at(load, tick - LOAD_AT)
+            at(project, tick - PROJECT_AT)
+            at(turn, tick - TURN_AT)
+            at(subtract, tick - SUBTRACT_AT)
+            at(quantise, tick - QUANTISE_AT)
 
         dist = const.tile([P, SOURCES, TILES], F32)
         nearest = const.tile([P, TILES], F32)

@@ -26,12 +26,10 @@ GROUPS = TILES // GROUP_TILES
 HALVES = 2
 WORDS = HIDDEN // 2
 
-BLOCK_GROUPS = SOURCES
-
 LOAD_AT = 0
 TURN_AT = 4
-SUBTRACT_AT = TURN_AT + BLOCK_GROUPS + 1
-QUANTISE_AT = SUBTRACT_AT + BLOCK_GROUPS
+SUBTRACT_AT = TURN_AT + 2
+QUANTISE_AT = SUBTRACT_AT + 1
 PROJECT_AT = QUANTISE_AT + 1
 
 SQRT_FLOOR = 2.0 ** -116
@@ -71,41 +69,33 @@ def tile_moe_pa_t_e_kernel(tc, encodings, domain_encs, Us_words, Us_scales, out)
                     nc.tensor.transpose(
                         planes[:, u, h * P : (h + 1) * P], words[:, u:WORDS:HALVES], identity[:]
                     )
-            b, c = divmod(g, BLOCK_GROUPS)
-            if c == 0:
-                turned = turned_pool.tile([P, BLOCK_GROUPS, GROUP, PACK], BF16)
-                turned_of[b] = turned
+            turned = turned_pool.tile([P, GROUP, PACK], BF16)
             nc.scalar.copy(
-                out=turned_of[b][:, c, :, :]
+                out=turned[:]
                 .rearrange("p n t -> p (n t)")
                 .bitcast(F32)
                 .rearrange("p (n u) -> p n u", u=HALVES),
                 in_=planes[:].rearrange("p u n -> p n u"),
             )
+            turned_of[g] = turned
 
         def subtract(g):
-            b, s = divmod(g, SOURCES)
-            if s == 0:
-                diff = diff_pool.tile([P, BLOCK_GROUPS, SOURCES, GROUP, PACK], BF16, align_bytes=64)
-                diff_of[b] = diff
+            diff = diff_pool.tile([P, SOURCES, GROUP, PACK], BF16, align_bytes=64)
             nc.vector.tensor_tensor(
-                out=diff_of[b][:, :, s, :, :],
-                in0=turned_of[b][:],
-                in1=dom_t[:, s, :]
-                .unsqueeze(1)
-                .unsqueeze(1)
-                .to_broadcast([P, BLOCK_GROUPS, GROUP, PACK]),
+                out=diff[:],
+                in0=turned_of[g][:].unsqueeze(1).to_broadcast([P, SOURCES, GROUP, PACK]),
+                in1=dom_t[:].unsqueeze(2).to_broadcast([P, SOURCES, GROUP, PACK]),
                 op=ALU.subtract,
             )
+            diff_of[g] = diff
 
         def quantise(g):
-            b, c = divmod(g, BLOCK_GROUPS)
             codes = code_pool.tile([P, SOURCES, GROUP], U32, align_bytes=64)
             scales = code_pool.tile([P, SOURCES, GROUP], U8, align_bytes=64)
             nc.vector.quantize_mx(
                 out=codes[:].rearrange("p s n -> p (s n)").bitcast(FP8X4),
                 scales=scales[:].rearrange("p s n -> p (s n)"),
-                in_=diff_of[b][:, c, :, :, :].rearrange("p s n t -> p (s n t)"),
+                in_=diff_of[g][:].rearrange("p s n t -> p (s n t)"),
             )
             codes_of[g], scales_of[g] = codes, scales
 
@@ -162,7 +152,7 @@ def tile_moe_pa_t_e_kernel(tc, encodings, domain_encs, Us_words, Us_scales, out)
                 stage(g)
 
         for tick in range(GROUPS + PROJECT_AT):
-            if tick == BLOCK_GROUPS:
+            if tick == TURN_AT:
                 load_weights()
             at(load, tick - LOAD_AT)
             at(project, tick - PROJECT_AT)

@@ -47,7 +47,7 @@ def tile_moe_pa_t_e_kernel(tc, encodings, domain_encs, Us_words, Us_scales, out)
         const = ctx.enter_context(tc.tile_pool(name="const", bufs=1))
         enc_pool = ctx.enter_context(tc.tile_pool(name="enc", bufs=TURN_AT + 2))
         turned_pool = ctx.enter_context(tc.tile_pool(name="turned", bufs=3))
-        diff_pool = ctx.enter_context(tc.tile_pool(name="diff", bufs=2))
+        diff_pool = ctx.enter_context(tc.tile_pool(name="diff", bufs=3))
         code_pool = ctx.enter_context(tc.tile_pool(name="code", bufs=3))
         square_pool = ctx.enter_context(tc.tile_pool(name="square", bufs=2))
         plane_pool = ctx.enter_context(tc.psum_pool(name="plane", bufs=3))

@@ -26,9 +26,13 @@ GROUPS = TILES // GROUP_TILES
 HALVES = 2
 WORDS = HIDDEN // 2
 
+HELPED_SOURCE = SOURCES - 1
+HELPED_FROM = GROUP - P
+
 LOAD_AT = 0
 TURN_AT = 4
-SUBTRACT_AT = TURN_AT + 2
+HELP_AT = TURN_AT + 2
+SUBTRACT_AT = HELP_AT + 1
 QUANTISE_AT = SUBTRACT_AT + 1
 PROJECT_AT = QUANTISE_AT + 1
 
@@ -50,10 +54,10 @@ def tile_moe_pa_t_e_kernel(tc, encodings, domain_encs, Us_words, Us_scales, out)
         diff_pool = ctx.enter_context(tc.tile_pool(name="diff", bufs=3))
         code_pool = ctx.enter_context(tc.tile_pool(name="code", bufs=3))
         square_pool = ctx.enter_context(tc.tile_pool(name="square", bufs=2))
-        plane_pool = ctx.enter_context(tc.psum_pool(name="plane", bufs=3))
+        plane_pool = ctx.enter_context(tc.psum_pool(name="plane", bufs=SUBTRACT_AT - TURN_AT + 1))
         proj_pool = ctx.enter_context(tc.psum_pool(name="proj", bufs=2 * GROUP_TILES))
 
-        enc_of, turned_of, diff_of, codes_of, scales_of = {}, {}, {}, {}, {}
+        enc_of, planes_of, turned_of, diff_of, codes_of, scales_of = {}, {}, {}, {}, {}, {}
 
         def load(g):
             enc_sb = enc_pool.tile([P, GROUP_TILES, HIDDEN], BF16)
@@ -69,25 +73,41 @@ def tile_moe_pa_t_e_kernel(tc, encodings, domain_encs, Us_words, Us_scales, out)
                     nc.tensor.transpose(
                         planes[:, u, h * P : (h + 1) * P], words[:, u:WORDS:HALVES], identity[:]
                     )
-            turned = turned_pool.tile([P, GROUP, PACK], BF16)
+            planes_of[g] = planes
+            turned = turned_pool.tile([P, GROUP - HELPED_FROM, PACK], BF16)
             nc.scalar.copy(
                 out=turned[:]
                 .rearrange("p n t -> p (n t)")
                 .bitcast(F32)
                 .rearrange("p (n u) -> p n u", u=HALVES),
-                in_=planes[:].rearrange("p u n -> p n u"),
+                in_=planes[:, :, HELPED_FROM:].rearrange("p u n -> p n u"),
             )
             turned_of[g] = turned
 
-        def subtract(g):
+
+        def help_subtract(g):
             diff = diff_pool.tile([P, SOURCES, GROUP, PACK], BF16, align_bytes=64)
-            nc.vector.tensor_tensor(
-                out=diff[:],
-                in0=turned_of[g][:].unsqueeze(1).to_broadcast([P, SOURCES, GROUP, PACK]),
-                in1=dom_t[:].unsqueeze(2).to_broadcast([P, SOURCES, GROUP, PACK]),
+            nc.gpsimd.tensor_tensor(
+                out=diff[:, HELPED_SOURCE, HELPED_FROM:, :],
+                in0=turned_of[g][:],
+                in1=dom_t[:, HELPED_SOURCE, :]
+                .unsqueeze(1)
+                .to_broadcast([P, GROUP - HELPED_FROM, PACK]),
                 op=ALU.subtract,
             )
             diff_of[g] = diff
+
+        def subtract(g):
+            pairs = planes_of[g][:].bitcast(BF16).rearrange("p u (n e) -> p n u e", e=2)
+            for s in range(SOURCES):
+                count = HELPED_FROM if s == HELPED_SOURCE else GROUP
+                centre = dom_t[:, s, :].rearrange("p (u e) -> p u e", e=2).unsqueeze(1)
+                nc.vector.tensor_tensor(
+                    out=diff_of[g][:, s, :count, :].rearrange("p n (u e) -> p n u e", e=2),
+                    in0=pairs[:, :count],
+                    in1=centre.to_broadcast([P, count, HALVES, 2]),
+                    op=ALU.subtract,
+                )
 
         def quantise(g):
             codes = code_pool.tile([P, SOURCES, GROUP], U32, align_bytes=64)
@@ -157,6 +177,7 @@ def tile_moe_pa_t_e_kernel(tc, encodings, domain_encs, Us_words, Us_scales, out)
             at(load, tick - LOAD_AT)
             at(project, tick - PROJECT_AT)
             at(turn, tick - TURN_AT)
+            at(help_subtract, tick - HELP_AT)
             at(subtract, tick - SUBTRACT_AT)
             at(quantise, tick - QUANTISE_AT)
 

@@ -27,7 +27,8 @@ HALVES = 2
 WORDS = HIDDEN // 2
 
 HELPED_SOURCE = SOURCES - 1
-HELPED_FROM = GROUP - P
+HELPED_TOKENS = 160
+HELPED_FROM = GROUP - HELPED_TOKENS
 
 LOAD_AT = 0
 TURN_AT = 4
@@ -74,7 +75,7 @@ def tile_moe_pa_t_e_kernel(tc, encodings, domain_encs, Us_words, Us_scales, out)
                         planes[:, u, h * P : (h + 1) * P], words[:, u:WORDS:HALVES], identity[:]
                     )
             planes_of[g] = planes
-            turned = turned_pool.tile([P, GROUP - HELPED_FROM, PACK], BF16)
+            turned = turned_pool.tile([P, HELPED_TOKENS, PACK], BF16)
             nc.scalar.copy(
                 out=turned[:]
                 .rearrange("p n t -> p (n t)")
@@ -92,7 +93,7 @@ def tile_moe_pa_t_e_kernel(tc, encodings, domain_encs, Us_words, Us_scales, out)
                 in0=turned_of[g][:],
                 in1=dom_t[:, HELPED_SOURCE, :]
                 .unsqueeze(1)
-                .to_broadcast([P, GROUP - HELPED_FROM, PACK]),
+                .to_broadcast([P, HELPED_TOKENS, PACK]),
                 op=ALU.subtract,
             )
             diff_of[g] = diff

@@ -29,9 +29,12 @@ WORDS = HIDDEN // 2
 HELPED_SOURCE = SOURCES - 1
 HELPED_TOKENS = 160
 HELPED_FROM = GROUP - HELPED_TOKENS
+MADE_TOKENS = HELPED_FROM
+assert MADE_TOKENS <= P
 
 LOAD_AT = 0
 TURN_AT = 4
+MAKE_AT = TURN_AT + 1
 HELP_AT = TURN_AT + 2
 SUBTRACT_AT = HELP_AT + 1
 QUANTISE_AT = SUBTRACT_AT + 1
@@ -56,9 +59,10 @@ def tile_moe_pa_t_e_kernel(tc, encodings, domain_encs, Us_words, Us_scales, out)
         code_pool = ctx.enter_context(tc.tile_pool(name="code", bufs=3))
         square_pool = ctx.enter_context(tc.tile_pool(name="square", bufs=2))
         plane_pool = ctx.enter_context(tc.psum_pool(name="plane", bufs=SUBTRACT_AT - TURN_AT + 1))
-        proj_pool = ctx.enter_context(tc.psum_pool(name="proj", bufs=2 * GROUP_TILES))
+        proj_pool = ctx.enter_context(tc.psum_pool(name="proj", bufs=GROUP_TILES))
+        made_pool = ctx.enter_context(tc.psum_pool(name="made", bufs=2))
 
-        enc_of, planes_of, turned_of, diff_of, codes_of, scales_of = {}, {}, {}, {}, {}, {}
+        enc_of, planes_of, turned_of, diff_of, codes_of, scales_of, made_of = {}, {}, {}, {}, {}, {}, {}
 
         def load(g):
             enc_sb = enc_pool.tile([P, GROUP_TILES, HIDDEN], BF16)
@@ -85,6 +89,33 @@ def tile_moe_pa_t_e_kernel(tc, encodings, domain_encs, Us_words, Us_scales, out)
             )
             turned_of[g] = turned
 
+        def make(g):
+            made = made_pool.tile([P, PACK, P], F32)
+            for t in range(PACK):
+                nc.tensor.matmul(
+                    out=made[:, t, :],
+                    lhsT=neg_centre[:, t, :],
+                    rhs=identity[:],
+                    is_transpose=True,
+                    start=(t == 0),
+                    stop=False,
+                )
+            for t in range(PACK):
+                nc.tensor.matmul(
+                    out=made[:, t, :MADE_TOKENS],
+                    lhsT=enc_of[g][:, 0, t:HIDDEN:PACK],
+                    rhs=identity_bf[:, :MADE_TOKENS],
+                    start=False,
+                    stop=(t == PACK - 1),
+                )
+            made_of[g] = made
+
+        def fetch(g):
+            nc.scalar.copy(
+                out=diff_of[g][:, HELPED_SOURCE, :MADE_TOKENS, :],
+                in_=made_of[g][:, :, :MADE_TOKENS].rearrange("p t n -> p n t"),
+            )
+
 
         def help_subtract(g):
             diff = diff_pool.tile([P, SOURCES, GROUP, PACK], BF16, align_bytes=64)
@@ -100,8 +131,8 @@ def tile_moe_pa_t_e_kernel(tc, encodings, domain_encs, Us_words, Us_scales, out)
 
         def subtract(g):
             pairs = planes_of[g][:].bitcast(BF16).rearrange("p u (n e) -> p n u e", e=2)
-            for s in range(SOURCES):
-                count = HELPED_FROM if s == HELPED_SOURCE else GROUP
+            for s in range(HELPED_SOURCE):
+                count = GROUP
                 centre = dom_t[:, s, :].rearrange("p (u e) -> p u e", e=2).unsqueeze(1)
                 nc.vector.tensor_tensor(
                     out=diff_of[g][:, s, :count, :].rearrange("p n (u e) -> p n u e", e=2),
@@ -148,6 +179,10 @@ def tile_moe_pa_t_e_kernel(tc, encodings, domain_encs, Us_words, Us_scales, out)
         nc.sync.dma_start(out=dom_t[:], in_=domain_encs.rearrange("s (p t) -> p s t", t=PACK))
         identity = const.tile([P, P], F32)
         make_identity(nc, identity[:])
+        identity_bf = const.tile([P, P], BF16)
+        make_identity(nc, identity_bf[:])
+        centre_rows = const.tile([P, HIDDEN], BF16)
+        neg_centre = const.tile([P, PACK, P], F32)
         warm = const.tile([P, 1], F32)
         nc.vector.memset(warm[:], 1.0)
         nc.scalar.activation(out=warm[:], in_=warm[:], func=ACT.Sqrt)
@@ -176,9 +211,20 @@ def tile_moe_pa_t_e_kernel(tc, encodings, domain_encs, Us_words, Us_scales, out)
             if tick == TURN_AT:
                 load_weights()
             at(load, tick - LOAD_AT)
+            if tick == 1:
+                nc.sync.dma_start(
+                    out=centre_rows[:], in_=domain_encs[HELPED_SOURCE].partition_broadcast(P)
+                )
+                nc.scalar.mul(
+                    out=neg_centre[:],
+                    in_=centre_rows[:].rearrange("p (m t) -> p t m", t=PACK),
+                    mul=-1.0,
+                )
             at(project, tick - PROJECT_AT)
             at(turn, tick - TURN_AT)
+            at(make, tick - MAKE_AT)
             at(help_subtract, tick - HELP_AT)
+            at(fetch, tick - HELP_AT)
             at(subtract, tick - SUBTRACT_AT)
             at(quantise, tick - QUANTISE_AT)
 

@@ -27,10 +27,10 @@ HALVES = 2
 WORDS = HIDDEN // 2
 
 HELPED_SOURCE = SOURCES - 1
-HELPED_TOKENS = 160
+HELPED_TOKENS = 132
 HELPED_FROM = GROUP - HELPED_TOKENS
-MADE_TOKENS = HELPED_FROM
-assert MADE_TOKENS <= P
+MADE_TOKENS = 96
+assert MADE_TOKENS <= HELPED_FROM and MADE_TOKENS <= P
 
 LOAD_AT = 0
 TURN_AT = 4
@@ -131,12 +131,13 @@ def tile_moe_pa_t_e_kernel(tc, encodings, domain_encs, Us_words, Us_scales, out)
 
         def subtract(g):
             pairs = planes_of[g][:].bitcast(BF16).rearrange("p u (n e) -> p n u e", e=2)
-            for s in range(HELPED_SOURCE):
-                count = GROUP
+            for s in range(SOURCES):
+                mine = slice(MADE_TOKENS, HELPED_FROM) if s == HELPED_SOURCE else slice(0, GROUP)
+                count = mine.stop - mine.start
                 centre = dom_t[:, s, :].rearrange("p (u e) -> p u e", e=2).unsqueeze(1)
                 nc.vector.tensor_tensor(
-                    out=diff_of[g][:, s, :count, :].rearrange("p n (u e) -> p n u e", e=2),
-                    in0=pairs[:, :count],
+                    out=diff_of[g][:, s, mine, :].rearrange("p n (u e) -> p n u e", e=2),
+                    in0=pairs[:, mine],
                     in1=centre.to_broadcast([P, count, HALVES, 2]),
                     op=ALU.subtract,
                 )

@@ -27,10 +27,11 @@ HALVES = 2
 WORDS = HIDDEN // 2
 
 HELPED_SOURCE = SOURCES - 1
-HELPED_TOKENS = 132
+HELPED_TOKENS = 156
 HELPED_FROM = GROUP - HELPED_TOKENS
-MADE_TOKENS = 96
+MADE_TOKENS = 100
 assert MADE_TOKENS <= HELPED_FROM and MADE_TOKENS <= P
+CUE_TOKENS = 4
 
 LOAD_AT = 0
 TURN_AT = 4
@@ -117,30 +118,38 @@ def tile_moe_pa_t_e_kernel(tc, encodings, domain_encs, Us_words, Us_scales, out)
             )
 
 
-        def help_subtract(g):
+        def open_diff(g):
             diff = diff_pool.tile([P, SOURCES, GROUP, PACK], BF16, align_bytes=64)
+            diff_of[g] = diff
+
+        def help_subtract(g):
             nc.gpsimd.tensor_tensor(
-                out=diff[:, HELPED_SOURCE, HELPED_FROM:, :],
+                out=diff_of[g][:, HELPED_SOURCE, HELPED_FROM:, :],
                 in0=turned_of[g][:],
                 in1=dom_t[:, HELPED_SOURCE, :]
                 .unsqueeze(1)
                 .to_broadcast([P, HELPED_TOKENS, PACK]),
                 op=ALU.subtract,
             )
-            diff_of[g] = diff
 
         def subtract(g):
             pairs = planes_of[g][:].bitcast(BF16).rearrange("p u (n e) -> p n u e", e=2)
-            for s in range(SOURCES):
-                mine = slice(MADE_TOKENS, HELPED_FROM) if s == HELPED_SOURCE else slice(0, GROUP)
-                count = mine.stop - mine.start
-                centre = dom_t[:, s, :].rearrange("p (u e) -> p u e", e=2).unsqueeze(1)
-                nc.vector.tensor_tensor(
-                    out=diff_of[g][:, s, mine, :].rearrange("p n (u e) -> p n u e", e=2),
-                    in0=pairs[:, mine],
-                    in1=centre.to_broadcast([P, count, HALVES, 2]),
-                    op=ALU.subtract,
-                )
+            for s in range(HELPED_SOURCE):
+                subtract_part(g, pairs, s, slice(0, GROUP))
+
+        def cue(g):
+            pairs = planes_of[g][:].bitcast(BF16).rearrange("p u (n e) -> p n u e", e=2)
+            subtract_part(g, pairs, HELPED_SOURCE, slice(MADE_TOKENS, HELPED_FROM + CUE_TOKENS))
+
+        def subtract_part(g, pairs, s, mine):
+            count = mine.stop - mine.start
+            centre = dom_t[:, s, :].rearrange("p (u e) -> p u e", e=2).unsqueeze(1)
+            nc.vector.tensor_tensor(
+                out=diff_of[g][:, s, mine, :].rearrange("p n (u e) -> p n u e", e=2),
+                in0=pairs[:, mine],
+                in1=centre.to_broadcast([P, count, HALVES, 2]),
+                op=ALU.subtract,
+            )
 
         def quantise(g):
             codes = code_pool.tile([P, SOURCES, GROUP], U32, align_bytes=64)
@@ -224,9 +233,11 @@ def tile_moe_pa_t_e_kernel(tc, encodings, domain_encs, Us_words, Us_scales, out)
             at(project, tick - PROJECT_AT)
             at(turn, tick - TURN_AT)
             at(make, tick - MAKE_AT)
+            at(open_diff, tick - HELP_AT)
+            at(subtract, tick - SUBTRACT_AT)
+            at(cue, tick - HELP_AT)
             at(help_subtract, tick - HELP_AT)
             at(fetch, tick - HELP_AT)
-            at(subtract, tick - SUBTRACT_AT)
             at(quantise, tick - QUANTISE_AT)
 
         dist = const.tile([P, SOURCES, TILES], F32)

@@ -191,8 +191,19 @@ def tile_moe_pa_t_e_kernel(tc, encodings, domain_encs, Us_words, Us_scales, out)
         make_identity(nc, identity[:])
         identity_bf = const.tile([P, P], BF16)
         make_identity(nc, identity_bf[:])
-        centre_rows = const.tile([P, HIDDEN], BF16)
+        neg_dom = const.tile([P, PACK], F32)
         neg_centre = const.tile([P, PACK, P], F32)
+
+        def spread_centre():
+            nc.vector.tensor_scalar_mul(
+                out=neg_dom[:], in0=dom_t[:, HELPED_SOURCE, :], scalar1=-1.0
+            )
+            made = made_pool.tile([P, PACK, P], F32)
+            for t in range(PACK):
+                nc.tensor.transpose(
+                    made[:, t, :], neg_dom[:, t : t + 1].to_broadcast([P, P]), identity[:]
+                )
+            nc.scalar.copy(out=neg_centre[:], in_=made[:])
         warm = const.tile([P, 1], F32)
         nc.vector.memset(warm[:], 1.0)
         nc.scalar.activation(out=warm[:], in_=warm[:], func=ACT.Sqrt)
@@ -221,17 +232,10 @@ def tile_moe_pa_t_e_kernel(tc, encodings, domain_encs, Us_words, Us_scales, out)
             if tick == TURN_AT:
                 load_weights()
             at(load, tick - LOAD_AT)
-            if tick == 1:
-                nc.sync.dma_start(
-                    out=centre_rows[:], in_=domain_encs[HELPED_SOURCE].partition_broadcast(P)
-                )
-                nc.scalar.mul(
-                    out=neg_centre[:],
-                    in_=centre_rows[:].rearrange("p (m t) -> p t m", t=PACK),
-                    mul=-1.0,
-                )
             at(project, tick - PROJECT_AT)
             at(turn, tick - TURN_AT)
+            if tick == TURN_AT:
+                spread_centre()
             at(make, tick - MAKE_AT)
             at(open_diff, tick - HELP_AT)
             at(subtract, tick - SUBTRACT_AT)

@@ -72,12 +72,12 @@ def tile_moe_pa_t_e_kernel(tc, encodings, domain_encs, Us_words, Us_scales, out)
             enc_of[g] = enc_sb
 
         def turn(g):
-            planes = plane_pool.tile([P, HALVES, GROUP], F32)
+            planes = plane_pool.tile([P, GROUP, HALVES], F32)
             for h in range(GROUP_TILES):
                 words = enc_of[g][:, h, :].bitcast(F32)
                 for u in range(HALVES):
                     nc.tensor.transpose(
-                        planes[:, u, h * P : (h + 1) * P], words[:, u:WORDS:HALVES], identity[:]
+                        planes[:, h * P : (h + 1) * P, u], words[:, u:WORDS:HALVES], identity[:]
                     )
             planes_of[g] = planes
             turned = turned_pool.tile([P, HELPED_TOKENS, PACK], BF16)
@@ -86,7 +86,7 @@ def tile_moe_pa_t_e_kernel(tc, encodings, domain_encs, Us_words, Us_scales, out)
                 .rearrange("p n t -> p (n t)")
                 .bitcast(F32)
                 .rearrange("p (n u) -> p n u", u=HALVES),
-                in_=planes[:, :, HELPED_FROM:].rearrange("p u n -> p n u"),
+                in_=planes[:, HELPED_FROM:, :],
             )
             turned_of[g] = turned
 
@@ -133,21 +133,23 @@ def tile_moe_pa_t_e_kernel(tc, encodings, domain_encs, Us_words, Us_scales, out)
             )
 
         def subtract(g):
-            pairs = planes_of[g][:].bitcast(BF16).rearrange("p u (n e) -> p n u e", e=2)
-            for s in range(HELPED_SOURCE):
-                subtract_part(g, pairs, s, slice(0, GROUP))
+            values = planes_of[g][:].rearrange("p n u -> p (n u)").bitcast(BF16)
+            shape = [P, HELPED_SOURCE, GROUP, PACK]
+            nc.vector.tensor_tensor(
+                out=diff_of[g][:, :HELPED_SOURCE, :, :],
+                in0=values.rearrange("p (n t) -> p n t", t=PACK).unsqueeze(1).to_broadcast(shape),
+                in1=dom_t[:, :HELPED_SOURCE, :].unsqueeze(2).to_broadcast(shape),
+                op=ALU.subtract,
+            )
 
         def cue(g):
-            pairs = planes_of[g][:].bitcast(BF16).rearrange("p u (n e) -> p n u e", e=2)
-            subtract_part(g, pairs, HELPED_SOURCE, slice(MADE_TOKENS, HELPED_FROM + CUE_TOKENS))
-
-        def subtract_part(g, pairs, s, mine):
+            values = planes_of[g][:].rearrange("p n u -> p (n u)").bitcast(BF16)
+            mine = slice(MADE_TOKENS, HELPED_FROM + CUE_TOKENS)
             count = mine.stop - mine.start
-            centre = dom_t[:, s, :].rearrange("p (u e) -> p u e", e=2).unsqueeze(1)
             nc.vector.tensor_tensor(
-                out=diff_of[g][:, s, mine, :].rearrange("p n (u e) -> p n u e", e=2),
-                in0=pairs[:, mine],
-                in1=centre.to_broadcast([P, count, HALVES, 2]),
+                out=diff_of[g][:, HELPED_SOURCE, mine, :],
+                in0=values.rearrange("p (n t) -> p n t", t=PACK)[:, mine, :],
+                in1=dom_t[:, HELPED_SOURCE, :].unsqueeze(1).to_broadcast([P, count, PACK]),
                 op=ALU.subtract,
             )
 

@@ -43,6 +43,10 @@ PROJECT_AT = QUANTISE_AT + 1
 
 SQRT_FLOOR = 2.0 ** -116
 
+LATE_GROUPS = 4
+EARLY_TILES = TILES - LATE_GROUPS * GROUP_TILES
+EARLY_AT = GROUPS - LATE_GROUPS - 1 + PROJECT_AT + 1
+
 FLOPS = 2 * SOURCES * TOKENS * HIDDEN * RANK
 
 
@@ -188,7 +192,7 @@ def tile_moe_pa_t_e_kernel(tc, encodings, domain_encs, Us_words, Us_scales, out)
                     )
 
         dom_t = const.tile([P, SOURCES, PACK], BF16)
-        nc.sync.dma_start(out=dom_t[:], in_=domain_encs.rearrange("s (p t) -> p s t", t=PACK))
+        nc.scalar.dma_start(out=dom_t[:], in_=domain_encs.rearrange("s (p t) -> p s t", t=PACK))
         identity = const.tile([P, P], F32)
         make_identity(nc, identity[:])
         identity_bf = const.tile([P, P], BF16)
@@ -226,6 +230,56 @@ def tile_moe_pa_t_e_kernel(tc, encodings, domain_encs, Us_words, Us_scales, out)
                     .bitcast(I32),
                 )
 
+        dist = const.tile([P, SOURCES, TILES], F32)
+        nearest = const.tile([P, TILES], F32)
+        weight = const.tile([P, SOURCES, TILES], F32)
+        total = const.tile([P, TILES], F32)
+        floor = const.tile([P, 1], F32)
+        nc.vector.memset(floor[:], SQRT_FLOOR)
+
+        def roots(tiles):
+            nc.scalar.activation(
+                out=dist[:, :, tiles], in_=dist_sq[:, :, tiles], func=ACT.Sqrt, bias=floor[:]
+            )
+
+        def shift(tiles):
+            count = tiles.stop - tiles.start
+            nc.vector.tensor_reduce(
+                out=nearest[:, tiles],
+                in_=dist[:, :, tiles].rearrange("p s j -> p j s"),
+                axis=AXIS_X,
+                op=ALU.min,
+            )
+            nc.vector.tensor_tensor(
+                out=dist[:, :, tiles],
+                in0=dist[:, :, tiles],
+                in1=nearest[:, tiles].unsqueeze(1).to_broadcast([P, SOURCES, count]),
+                op=ALU.subtract,
+            )
+
+        def weigh(tiles):
+            nc.scalar.activation(out=weight[:, :, tiles], in_=dist[:, :, tiles], func=ACT.Exp, scale=-1.0)
+
+        def share(tiles):
+            count = tiles.stop - tiles.start
+            nc.vector.tensor_reduce(
+                out=total[:, tiles],
+                in_=weight[:, :, tiles].rearrange("p s j -> p j s"),
+                axis=AXIS_X,
+                op=ALU.add,
+            )
+            nc.vector.reciprocal(out=total[:, tiles], in_=total[:, tiles])
+            nc.vector.tensor_tensor(
+                out=weight[:, :, tiles],
+                in0=weight[:, :, tiles],
+                in1=total[:, tiles].unsqueeze(1).to_broadcast([P, SOURCES, count]),
+                op=ALU.mult,
+            )
+            nc.sync.dma_start(out=out_cols[:, :, tiles], in_=weight[:, :, tiles])
+
+        early = slice(0, EARLY_TILES)
+        late = slice(EARLY_TILES, TILES)
+
         def at(stage, g):
             if 0 <= g < GROUPS:
                 stage(g)
@@ -241,35 +295,20 @@ def tile_moe_pa_t_e_kernel(tc, encodings, domain_encs, Us_words, Us_scales, out)
             at(make, tick - MAKE_AT)
             at(open_diff, tick - HELP_AT)
             at(subtract, tick - SUBTRACT_AT)
+            if tick - SUBTRACT_AT == GROUPS - 2:
+                quantise(tick - QUANTISE_AT)
             at(cue, tick - HELP_AT)
             at(help_subtract, tick - HELP_AT)
             at(fetch, tick - HELP_AT)
-            at(quantise, tick - QUANTISE_AT)
+            if tick - SUBTRACT_AT == GROUPS - 2:
+                quantise(tick - QUANTISE_AT + 1)
+            elif tick - SUBTRACT_AT != GROUPS - 1:
+                at(quantise, tick - QUANTISE_AT)
+            if tick == EARLY_AT:
+                roots(early)
 
-        dist = const.tile([P, SOURCES, TILES], F32)
-        nearest = const.tile([P, TILES], F32)
-        weight = const.tile([P, SOURCES, TILES], F32)
-        total = const.tile([P, TILES], F32)
-        nc.vector.tensor_scalar_max(out=dist_sq[:], in0=dist_sq[:], scalar1=SQRT_FLOOR)
-        nc.scalar.activation(out=dist[:], in_=dist_sq[:], func=ACT.Sqrt)
-        nc.vector.tensor_reduce(
-            out=nearest[:], in_=dist[:].rearrange("p s j -> p j s"), axis=AXIS_X, op=ALU.min
-        )
-        nc.vector.tensor_tensor(
-            out=dist[:],
-            in0=dist[:],
-            in1=nearest[:].unsqueeze(1).to_broadcast([P, SOURCES, TILES]),
-            op=ALU.subtract,
-        )
-        nc.scalar.activation(out=weight[:], in_=dist[:], func=ACT.Exp, scale=-1.0)
-        nc.vector.tensor_reduce(
-            out=total[:], in_=weight[:].rearrange("p s j -> p j s"), axis=AXIS_X, op=ALU.add
-        )
-        nc.vector.reciprocal(out=total[:], in_=total[:])
-        nc.vector.tensor_tensor(
-            out=weight[:],
-            in0=weight[:],
-            in1=total[:].unsqueeze(1).to_broadcast([P, SOURCES, TILES]),
-            op=ALU.mult,
-        )
-        nc.sync.dma_start(out=out_cols, in_=weight[:])
+        shift(early)
+        roots(late)
+        shift(late)
+        weigh(slice(0, TILES))
+        share(slice(0, TILES))

@@ -22,32 +22,31 @@ assert HIDDEN == P * PACK
 TILES = TOKENS // P
 GROUP_TILES = 2
 GROUP = GROUP_TILES * P
-GROUPS = TILES // GROUP_TILES
+PAIR_GROUPS = 2
+PAIR_TILES = PAIR_GROUPS * GROUP_TILES
+PAIRS = TILES // PAIR_TILES
 HALVES = 2
 WORDS = HIDDEN // 2
 
-HELPED_SOURCE = SOURCES - 1
-HELPED_TOKENS = 156
-HELPED_FROM = GROUP - HELPED_TOKENS
-MADE_TOKENS = 100
-assert MADE_TOKENS <= HELPED_FROM and MADE_TOKENS <= P
-CUE_TOKENS = 4
+HELPED = 80
+HELPED_FROM = GROUP - HELPED
+MADE = 51
+MADE_ROWS = 64
+MADE_TILES = 3
 
-LOAD_AT = 0
-TURN_AT = 4
-MAKE_AT = TURN_AT + 1
-HELP_AT = TURN_AT + 2
-SUBTRACT_AT = HELP_AT + 1
-QUANTISE_AT = SUBTRACT_AT + 1
-PROJECT_AT = QUANTISE_AT + 1
+FLOPS = 2 * SOURCES * TOKENS * HIDDEN * RANK
 
 SQRT_FLOOR = 2.0 ** -116
 
-LATE_GROUPS = 4
-EARLY_TILES = TILES - LATE_GROUPS * GROUP_TILES
-EARLY_AT = GROUPS - LATE_GROUPS - 1 + PROJECT_AT + 1
+LATE_PAIRS = 2
+EARLY_TILES = TILES - LATE_PAIRS * PAIR_TILES
 
-FLOPS = 2 * SOURCES * TOKENS * HIDDEN * RANK
+LOAD_AT = 0
+TURN_AT = 2
+SUBTRACT_AT = TURN_AT + 1
+QUANTISE_AT = SUBTRACT_AT + 1
+PROJECT_AT = QUANTISE_AT + 1
+EARLY_AT = PAIRS - LATE_PAIRS - 1 + PROJECT_AT + 1
 
 
 def tile_moe_pa_t_e_kernel(tc, encodings, domain_encs, Us_words, Us_scales, out):
@@ -58,22 +57,28 @@ def tile_moe_pa_t_e_kernel(tc, encodings, domain_encs, Us_words, Us_scales, out)
     with ExitStack() as ctx:
         ctx.enter_context(tc.manual_schedule())
         const = ctx.enter_context(tc.tile_pool(name="const", bufs=1))
-        enc_pool = ctx.enter_context(tc.tile_pool(name="enc", bufs=TURN_AT + 2))
-        turned_pool = ctx.enter_context(tc.tile_pool(name="turned", bufs=3))
-        diff_pool = ctx.enter_context(tc.tile_pool(name="diff", bufs=3))
-        code_pool = ctx.enter_context(tc.tile_pool(name="code", bufs=3))
+        enc_pool = ctx.enter_context(tc.tile_pool(name="enc", bufs=2 * (TURN_AT + 2)))
+        turned_pool = ctx.enter_context(tc.tile_pool(name="turned", bufs=2))
+        diff_pool = ctx.enter_context(tc.tile_pool(name="diff", bufs=2))
+        code_pool = ctx.enter_context(tc.tile_pool(name="code", bufs=6))
         square_pool = ctx.enter_context(tc.tile_pool(name="square", bufs=2))
-        plane_pool = ctx.enter_context(tc.psum_pool(name="plane", bufs=SUBTRACT_AT - TURN_AT + 1))
-        proj_pool = ctx.enter_context(tc.psum_pool(name="proj", bufs=GROUP_TILES))
-        made_pool = ctx.enter_context(tc.psum_pool(name="made", bufs=2))
+        plane_pool = ctx.enter_context(tc.psum_pool(name="plane", bufs=4))
+        proj_pool = ctx.enter_context(tc.psum_pool(name="proj", bufs=2))
+        made_pool = ctx.enter_context(tc.psum_pool(name="made", bufs=1))
 
-        enc_of, planes_of, turned_of, diff_of, codes_of, scales_of, made_of = {}, {}, {}, {}, {}, {}, {}
+        enc_of, planes_of, turned_of, diff_of, codes_of, scales_of = {}, {}, {}, {}, {}, {}
 
         def load(g):
             enc_sb = enc_pool.tile([P, GROUP_TILES, HIDDEN], BF16)
             first = g * GROUP_TILES
             nc.sync.dma_start(out=enc_sb[:], in_=enc_rows[:, first : first + GROUP_TILES, :])
             enc_of[g] = enc_sb
+
+        def load_made(q):
+            nc.sync.dma_start(
+                out=made_rows[q % MADE_TILES][:MADE_ROWS, :],
+                in_=enc_rows[:MADE_ROWS, q * PAIR_TILES + GROUP_TILES, :],
+            )
 
         def turn(g):
             planes = plane_pool.tile([P, GROUP, HALVES], F32)
@@ -84,76 +89,56 @@ def tile_moe_pa_t_e_kernel(tc, encodings, domain_encs, Us_words, Us_scales, out)
                         planes[:, h * P : (h + 1) * P, u], words[:, u:WORDS:HALVES], identity[:]
                     )
             planes_of[g] = planes
-            turned = turned_pool.tile([P, HELPED_TOKENS, PACK], BF16)
+
+        def hand_over(g):
+            turned = turned_pool.tile([P, HELPED, PACK], BF16)
             nc.scalar.copy(
                 out=turned[:]
                 .rearrange("p n t -> p (n t)")
                 .bitcast(F32)
                 .rearrange("p (n u) -> p n u", u=HALVES),
-                in_=planes[:, HELPED_FROM:, :],
+                in_=planes_of[g][:, HELPED_FROM:, :],
             )
             turned_of[g] = turned
 
-        def make(g):
-            made = made_pool.tile([P, PACK, P], F32)
+        def make(q):
+            made = made_pool.tile([P, PACK, SOURCES * MADE], BF16)
             for t in range(PACK):
                 nc.tensor.matmul(
                     out=made[:, t, :],
-                    lhsT=neg_centre[:, t, :],
-                    rhs=identity[:],
-                    is_transpose=True,
-                    start=(t == 0),
-                    stop=False,
+                    lhsT=made_rows[q % MADE_TILES][:, t:HIDDEN:PACK],
+                    rhs=chooser[:].rearrange("p s n -> p (s n)"),
+                    start=True,
+                    stop=True,
                 )
-            for t in range(PACK):
-                nc.tensor.matmul(
-                    out=made[:, t, :MADE_TOKENS],
-                    lhsT=enc_of[g][:, 0, t:HIDDEN:PACK],
-                    rhs=identity_bf[:, :MADE_TOKENS],
-                    start=False,
-                    stop=(t == PACK - 1),
-                )
-            made_of[g] = made
-
-        def fetch(g):
             nc.scalar.copy(
-                out=diff_of[g][:, HELPED_SOURCE, :MADE_TOKENS, :],
-                in_=made_of[g][:, :, :MADE_TOKENS].rearrange("p t n -> p n t"),
+                out=diff_of[2 * q + 1][:, :, :MADE, :],
+                in_=made[:].rearrange("p t (s n) -> p s n t", s=SOURCES),
             )
 
-
-        def open_diff(g):
-            diff = diff_pool.tile([P, SOURCES, GROUP, PACK], BF16, align_bytes=64)
-            diff_of[g] = diff
+        def open_diff(q):
+            first = diff_pool.tile([P, SOURCES, GROUP, PACK], BF16, align_bytes=64)
+            second = diff_pool.tile([P, SOURCES, GROUP, PACK], BF16, align_bytes=64)
+            diff_of[2 * q], diff_of[2 * q + 1] = first, second
 
         def help_subtract(g):
+            shape = [P, SOURCES, HELPED, PACK]
             nc.gpsimd.tensor_tensor(
-                out=diff_of[g][:, HELPED_SOURCE, HELPED_FROM:, :],
-                in0=turned_of[g][:],
-                in1=dom_t[:, HELPED_SOURCE, :]
+                out=diff_of[g][:, :, HELPED_FROM:, :],
+                in0=turned_of[g][:].unsqueeze(1).to_broadcast(shape),
+                in1=dom_t[:].unsqueeze(2).to_broadcast(shape),
+                op=ALU.subtract,
+            )
+
+        def subtract(g, tokens):
+            values = planes_of[g][:].rearrange("p n u -> p (n u)").bitcast(BF16)
+            shape = [P, SOURCES, tokens.stop - tokens.start, PACK]
+            nc.vector.tensor_tensor(
+                out=diff_of[g][:, :, tokens, :],
+                in0=values.rearrange("p (n t) -> p n t", t=PACK)[:, tokens, :]
                 .unsqueeze(1)
-                .to_broadcast([P, HELPED_TOKENS, PACK]),
-                op=ALU.subtract,
-            )
-
-        def subtract(g):
-            values = planes_of[g][:].rearrange("p n u -> p (n u)").bitcast(BF16)
-            shape = [P, HELPED_SOURCE, GROUP, PACK]
-            nc.vector.tensor_tensor(
-                out=diff_of[g][:, :HELPED_SOURCE, :, :],
-                in0=values.rearrange("p (n t) -> p n t", t=PACK).unsqueeze(1).to_broadcast(shape),
-                in1=dom_t[:, :HELPED_SOURCE, :].unsqueeze(2).to_broadcast(shape),
-                op=ALU.subtract,
-            )
-
-        def cue(g):
-            values = planes_of[g][:].rearrange("p n u -> p (n u)").bitcast(BF16)
-            mine = slice(MADE_TOKENS, HELPED_FROM + CUE_TOKENS)
-            count = mine.stop - mine.start
-            nc.vector.tensor_tensor(
-                out=diff_of[g][:, HELPED_SOURCE, mine, :],
-                in0=values.rearrange("p (n t) -> p n t", t=PACK)[:, mine, :],
-                in1=dom_t[:, HELPED_SOURCE, :].unsqueeze(1).to_broadcast([P, count, PACK]),
+                .to_broadcast(shape),
+                in1=dom_t[:].unsqueeze(2).to_broadcast(shape),
                 op=ALU.subtract,
             )
 
@@ -167,29 +152,28 @@ def tile_moe_pa_t_e_kernel(tc, encodings, domain_encs, Us_words, Us_scales, out)
             )
             codes_of[g], scales_of[g] = codes, scales
 
-        def project(g):
-            squares = square_pool.tile([P, GROUP_TILES, SOURCES, RANK], F32)
-            for h in range(GROUP_TILES):
-                proj = proj_pool.tile([P, SOURCES, RANK], F32)
-                tokens = slice(h * P, (h + 1) * P)
-                for s in range(SOURCES):
-                    nc.tensor.matmul_mx(
-                        out=proj[:, s, :],
-                        lhsT=codes_of[g][:, s, tokens].bitcast(FP8X4),
-                        lhsT_scale=scales_of[g][:, s, tokens],
-                        rhs=u_words[:, s, :].bitcast(FP4X4),
-                        rhs_scale=u_scales[:, s, :],
-                        start=True,
-                        stop=True,
-                    )
-                j = g * GROUP_TILES + h
-                for s in range(SOURCES):
-                    nc.scalar.activation(
-                        out=squares[:, h, s, :],
-                        in_=proj[:, s, :],
-                        func=ACT.Square,
-                        accum_out=dist_sq[:, s, j : j + 1],
-                    )
+        def project(j):
+            g, h = j // GROUP_TILES, j % GROUP_TILES
+            squares = square_pool.tile([P, SOURCES, RANK], F32)
+            proj = proj_pool.tile([P, SOURCES, RANK], F32)
+            tokens = slice(h * P, (h + 1) * P)
+            for s in range(SOURCES):
+                nc.tensor.matmul_mx(
+                    out=proj[:, s, :],
+                    lhsT=codes_of[g][:, s, tokens].bitcast(FP8X4),
+                    lhsT_scale=scales_of[g][:, s, tokens],
+                    rhs=u_words[:, s, :].bitcast(FP4X4),
+                    rhs_scale=u_scales[:, s, :],
+                    start=True,
+                    stop=True,
+                )
+            for s in range(SOURCES):
+                nc.scalar.activation(
+                    out=squares[:, s, :],
+                    in_=proj[:, s, :],
+                    func=ACT.Square,
+                    accum_out=dist_sq[:, s, j : j + 1],
+                )
 
         dom_t = const.tile([P, SOURCES, PACK], BF16)
         nc.scalar.dma_start(out=dom_t[:], in_=domain_encs.rearrange("s (p t) -> p s t", t=PACK))
@@ -197,19 +181,21 @@ def tile_moe_pa_t_e_kernel(tc, encodings, domain_encs, Us_words, Us_scales, out)
         make_identity(nc, identity[:])
         identity_bf = const.tile([P, P], BF16)
         make_identity(nc, identity_bf[:])
-        neg_dom = const.tile([P, PACK], F32)
-        neg_centre = const.tile([P, PACK, P], F32)
-
-        def spread_centre():
-            nc.vector.tensor_scalar_mul(
-                out=neg_dom[:], in0=dom_t[:, HELPED_SOURCE, :], scalar1=-1.0
-            )
-            made = made_pool.tile([P, PACK, P], F32)
-            for t in range(PACK):
-                nc.tensor.transpose(
-                    made[:, t, :], neg_dom[:, t : t + 1].to_broadcast([P, P]), identity[:]
-                )
-            nc.scalar.copy(out=neg_centre[:], in_=made[:])
+        made_rows = []
+        for i in range(MADE_TILES):
+            rows = const.tile([P, HIDDEN], BF16, name="made_rows%d" % i)
+            nc.vector.memset(rows[:].bitcast(I32), 0)
+            nc.scalar.dma_start(out=rows[MADE_ROWS : MADE_ROWS + SOURCES, :], in_=domain_encs)
+            made_rows.append(rows)
+        chooser = const.tile([P, SOURCES, MADE], BF16)
+        nc.gpsimd.tensor_tensor(
+            out=chooser[:],
+            in0=identity_bf[:, :MADE].unsqueeze(1).to_broadcast([P, SOURCES, MADE]),
+            in1=identity_bf[:, MADE_ROWS : MADE_ROWS + SOURCES]
+            .unsqueeze(2)
+            .to_broadcast([P, SOURCES, MADE]),
+            op=ALU.subtract,
+        )
         warm = const.tile([P, 1], F32)
         nc.vector.memset(warm[:], 1.0)
         nc.scalar.activation(out=warm[:], in_=warm[:], func=ACT.Sqrt)
@@ -280,32 +266,47 @@ def tile_moe_pa_t_e_kernel(tc, encodings, domain_encs, Us_words, Us_scales, out)
         early = slice(0, EARLY_TILES)
         late = slice(EARLY_TILES, TILES)
 
-        def at(stage, g):
-            if 0 <= g < GROUPS:
-                stage(g)
-
-        for tick in range(GROUPS + PROJECT_AT):
+        for tick in range(PAIRS + PROJECT_AT):
+            loaded = tick - LOAD_AT
+            turned = tick - TURN_AT
+            subtracted = tick - SUBTRACT_AT
+            quantised = tick - QUANTISE_AT
+            projected = tick - PROJECT_AT
+            if 0 <= loaded < PAIRS:
+                load(2 * loaded)
+                load(2 * loaded + 1)
+            if 0 <= turned < PAIRS:
+                load_made(turned)
             if tick == TURN_AT:
                 load_weights()
-            at(load, tick - LOAD_AT)
-            at(project, tick - PROJECT_AT)
-            at(turn, tick - TURN_AT)
-            if tick == TURN_AT:
-                spread_centre()
-            at(make, tick - MAKE_AT)
-            at(open_diff, tick - HELP_AT)
-            at(subtract, tick - SUBTRACT_AT)
-            if tick - SUBTRACT_AT == GROUPS - 2:
-                quantise(tick - QUANTISE_AT)
-            at(cue, tick - HELP_AT)
-            at(help_subtract, tick - HELP_AT)
-            at(fetch, tick - HELP_AT)
-            if tick - SUBTRACT_AT == GROUPS - 2:
-                quantise(tick - QUANTISE_AT + 1)
-            elif tick - SUBTRACT_AT != GROUPS - 1:
-                at(quantise, tick - QUANTISE_AT)
+
+            def square_tile(i):
+                if 0 <= projected < PAIRS:
+                    project(projected * PAIR_TILES + i)
+
+            square_tile(0)
+            if 0 <= turned < PAIRS:
+                turn(2 * turned)
+                hand_over(2 * turned)
+            square_tile(1)
+            if 0 <= turned < PAIRS:
+                turn(2 * turned + 1)
+            square_tile(2)
+            if 0 <= subtracted < PAIRS:
+                make(subtracted)
+            square_tile(3)
             if tick == EARLY_AT:
                 roots(early)
+
+            if 0 <= subtracted < PAIRS:
+                subtract(2 * subtracted, slice(0, HELPED_FROM))
+                subtract(2 * subtracted + 1, slice(MADE, GROUP))
+            if 0 <= quantised < PAIRS:
+                quantise(2 * quantised)
+                quantise(2 * quantised + 1)
+            if 0 <= turned < PAIRS:
+                open_diff(turned)
+                help_subtract(2 * turned)
 
         shift(early)
         roots(late)

@@ -28,11 +28,13 @@ PAIRS = TILES // PAIR_TILES
 HALVES = 2
 WORDS = HIDDEN // 2
 
-HELPED = 80
+HELPED = 72
 HELPED_FROM = GROUP - HELPED
 MADE = 51
 MADE_ROWS = 64
 MADE_TILES = 3
+LIFTED_SOURCE = SOURCES - 1
+LIFTED_TILE = GROUP_TILES - 1
 
 FLOPS = 2 * SOURCES * TOKENS * HIDDEN * RANK
 
@@ -65,8 +67,10 @@ def tile_moe_pa_t_e_kernel(tc, encodings, domain_encs, Us_words, Us_scales, out)
         plane_pool = ctx.enter_context(tc.psum_pool(name="plane", bufs=4))
         proj_pool = ctx.enter_context(tc.psum_pool(name="proj", bufs=2))
         made_pool = ctx.enter_context(tc.psum_pool(name="made", bufs=1))
+        lifted_pool = ctx.enter_context(tc.psum_pool(name="lifted", bufs=1))
+        wide_pool = ctx.enter_context(tc.tile_pool(name="wide", bufs=2))
 
-        enc_of, planes_of, turned_of, diff_of, codes_of, scales_of = {}, {}, {}, {}, {}, {}
+        enc_of, planes_of, turned_of, diff_of, codes_of, scales_of, wide_of = {}, {}, {}, {}, {}, {}, {}
 
         def load(g):
             enc_sb = enc_pool.tile([P, GROUP_TILES, HIDDEN], BF16)
@@ -116,6 +120,31 @@ def tile_moe_pa_t_e_kernel(tc, encodings, domain_encs, Us_words, Us_scales, out)
                 in_=made[:].rearrange("p t (s n) -> p s n t", s=SOURCES),
             )
 
+        def widen(q):
+            wide = wide_pool.tile([P, PACK, P], F32)
+            nc.scalar.copy(
+                out=wide[:],
+                in_=enc_of[2 * q + 1][:, LIFTED_TILE, :].rearrange("n (p t) -> n t p", t=PACK),
+            )
+            wide_of[q] = wide
+
+        def lift(q):
+            lifted = lifted_pool.tile([P, PACK, P], F32)
+            for source, first in ((neg_centre, True), (wide_of[q], False)):
+                for t in range(PACK):
+                    nc.tensor.matmul(
+                        out=lifted[:, t, :],
+                        lhsT=source[:, t, :],
+                        rhs=identity[:],
+                        is_transpose=True,
+                        start=first and t == 0,
+                        stop=not first and t == PACK - 1,
+                    )
+            nc.scalar.copy(
+                out=diff_of[2 * q + 1][:, LIFTED_SOURCE, LIFTED_TILE * P :, :],
+                in_=lifted[:].rearrange("p t n -> p n t"),
+            )
+
         def open_diff(q):
             first = diff_pool.tile([P, SOURCES, GROUP, PACK], BF16, align_bytes=64)
             second = diff_pool.tile([P, SOURCES, GROUP, PACK], BF16, align_bytes=64)
@@ -130,15 +159,15 @@ def tile_moe_pa_t_e_kernel(tc, encodings, domain_encs, Us_words, Us_scales, out)
                 op=ALU.subtract,
             )
 
-        def subtract(g, tokens):
+        def subtract(g, tokens, sources):
             values = planes_of[g][:].rearrange("p n u -> p (n u)").bitcast(BF16)
-            shape = [P, SOURCES, tokens.stop - tokens.start, PACK]
+            shape = [P, sources, tokens.stop - tokens.start, PACK]
             nc.vector.tensor_tensor(
-                out=diff_of[g][:, :, tokens, :],
+                out=diff_of[g][:, :sources, tokens, :],
                 in0=values.rearrange("p (n t) -> p n t", t=PACK)[:, tokens, :]
                 .unsqueeze(1)
                 .to_broadcast(shape),
-                in1=dom_t[:].unsqueeze(2).to_broadcast(shape),
+                in1=dom_t[:, :sources, :].unsqueeze(2).to_broadcast(shape),
                 op=ALU.subtract,
             )
 
@@ -196,6 +225,20 @@ def tile_moe_pa_t_e_kernel(tc, encodings, domain_encs, Us_words, Us_scales, out)
             .to_broadcast([P, SOURCES, MADE]),
             op=ALU.subtract,
         )
+        neg_dom = const.tile([P, PACK], F32)
+        neg_centre = const.tile([P, PACK, P], F32)
+
+        def spread_centre():
+            nc.vector.tensor_scalar_mul(
+                out=neg_dom[:], in0=dom_t[:, LIFTED_SOURCE, :], scalar1=-1.0
+            )
+            lifted = lifted_pool.tile([P, PACK, P], F32)
+            for t in range(PACK):
+                nc.tensor.transpose(
+                    lifted[:, t, :], neg_dom[:, t : t + 1].to_broadcast([P, P]), identity[:]
+                )
+            nc.scalar.copy(out=neg_centre[:], in_=lifted[:])
+
         warm = const.tile([P, 1], F32)
         nc.vector.memset(warm[:], 1.0)
         nc.scalar.activation(out=warm[:], in_=warm[:], func=ACT.Sqrt)
@@ -291,16 +334,22 @@ def tile_moe_pa_t_e_kernel(tc, encodings, domain_encs, Us_words, Us_scales, out)
             square_tile(1)
             if 0 <= turned < PAIRS:
                 turn(2 * turned + 1)
+                widen(turned)
+            if tick == TURN_AT:
+                spread_centre()
             square_tile(2)
             if 0 <= subtracted < PAIRS:
                 make(subtracted)
             square_tile(3)
+            if 0 <= subtracted < PAIRS:
+                lift(subtracted)
             if tick == EARLY_AT:
                 roots(early)
 
             if 0 <= subtracted < PAIRS:
-                subtract(2 * subtracted, slice(0, HELPED_FROM))
-                subtract(2 * subtracted + 1, slice(MADE, GROUP))
+                subtract(2 * subtracted, slice(0, HELPED_FROM), SOURCES)
+                subtract(2 * subtracted + 1, slice(MADE, LIFTED_TILE * P), SOURCES)
+                subtract(2 * subtracted + 1, slice(LIFTED_TILE * P, GROUP), LIFTED_SOURCE)
             if 0 <= quantised < PAIRS:
                 quantise(2 * quantised)
                 quantise(2 * quantised + 1)

@@ -33,7 +33,8 @@ HELPED_FROM = GROUP - HELPED
 MADE = 51
 MADE_ROWS = 64
 MADE_TILES = 3
-LIFTED_SOURCE = SOURCES - 1
+LIFTED_SOURCES = 2
+WHOLE_SOURCES = SOURCES - LIFTED_SOURCES
 LIFTED_TILE = GROUP_TILES - 1
 
 FLOPS = 2 * SOURCES * TOKENS * HIDDEN * RANK
@@ -64,10 +65,10 @@ def tile_moe_pa_t_e_kernel(tc, encodings, domain_encs, Us_words, Us_scales, out)
         diff_pool = ctx.enter_context(tc.tile_pool(name="diff", bufs=2))
         code_pool = ctx.enter_context(tc.tile_pool(name="code", bufs=6))
         square_pool = ctx.enter_context(tc.tile_pool(name="square", bufs=2))
-        plane_pool = ctx.enter_context(tc.psum_pool(name="plane", bufs=4))
+        plane_pool = ctx.enter_context(tc.psum_pool(name="plane", bufs=3))
         proj_pool = ctx.enter_context(tc.psum_pool(name="proj", bufs=2))
         made_pool = ctx.enter_context(tc.psum_pool(name="made", bufs=1))
-        lifted_pool = ctx.enter_context(tc.psum_pool(name="lifted", bufs=1))
+        lifted_pool = ctx.enter_context(tc.psum_pool(name="lifted", bufs=2))
         wide_pool = ctx.enter_context(tc.tile_pool(name="wide", bufs=2))
 
         enc_of, planes_of, turned_of, diff_of, codes_of, scales_of, wide_of = {}, {}, {}, {}, {}, {}, {}
@@ -128,9 +129,9 @@ def tile_moe_pa_t_e_kernel(tc, encodings, domain_encs, Us_words, Us_scales, out)
             )
             wide_of[q] = wide
 
-        def lift(q):
+        def lift(q, s):
             lifted = lifted_pool.tile([P, PACK, P], F32)
-            for source, first in ((neg_centre, True), (wide_of[q], False)):
+            for source, first in ((neg_centre[s], True), (wide_of[q], False)):
                 for t in range(PACK):
                     nc.tensor.matmul(
                         out=lifted[:, t, :],
@@ -141,7 +142,7 @@ def tile_moe_pa_t_e_kernel(tc, encodings, domain_encs, Us_words, Us_scales, out)
                         stop=not first and t == PACK - 1,
                     )
             nc.scalar.copy(
-                out=diff_of[2 * q + 1][:, LIFTED_SOURCE, LIFTED_TILE * P :, :],
+                out=diff_of[2 * q + 1][:, s, LIFTED_TILE * P :, :],
                 in_=lifted[:].rearrange("p t n -> p n t"),
             )
 
@@ -225,19 +226,20 @@ def tile_moe_pa_t_e_kernel(tc, encodings, domain_encs, Us_words, Us_scales, out)
             .to_broadcast([P, SOURCES, MADE]),
             op=ALU.subtract,
         )
-        neg_dom = const.tile([P, PACK], F32)
-        neg_centre = const.tile([P, PACK, P], F32)
+        neg_dom = const.tile([P, SOURCES, PACK], F32)
+        neg_centre = {}
 
-        def spread_centre():
-            nc.vector.tensor_scalar_mul(
-                out=neg_dom[:], in0=dom_t[:, LIFTED_SOURCE, :], scalar1=-1.0
-            )
-            lifted = lifted_pool.tile([P, PACK, P], F32)
-            for t in range(PACK):
-                nc.tensor.transpose(
-                    lifted[:, t, :], neg_dom[:, t : t + 1].to_broadcast([P, P]), identity[:]
-                )
-            nc.scalar.copy(out=neg_centre[:], in_=lifted[:])
+        def spread_centres():
+            nc.vector.tensor_scalar_mul(out=neg_dom[:], in0=dom_t[:], scalar1=-1.0)
+            for s in range(WHOLE_SOURCES, SOURCES):
+                lifted = lifted_pool.tile([P, PACK, P], F32)
+                for t in range(PACK):
+                    nc.tensor.transpose(
+                        lifted[:, t, :], neg_dom[:, s, t : t + 1].to_broadcast([P, P]), identity[:]
+                    )
+                centre = const.tile([P, PACK, P], F32, name="centre%d" % s)
+                nc.scalar.copy(out=centre[:], in_=lifted[:])
+                neg_centre[s] = centre
 
         warm = const.tile([P, 1], F32)
         nc.vector.memset(warm[:], 1.0)
@@ -327,29 +329,30 @@ def tile_moe_pa_t_e_kernel(tc, encodings, domain_encs, Us_words, Us_scales, out)
                 if 0 <= projected < PAIRS:
                     project(projected * PAIR_TILES + i)
 
+            if 0 <= subtracted < PAIRS:
+                subtract(2 * subtracted, slice(0, HELPED_FROM), SOURCES)
+                subtract(2 * subtracted + 1, slice(MADE, LIFTED_TILE * P), SOURCES)
+                subtract(2 * subtracted + 1, slice(LIFTED_TILE * P, GROUP), WHOLE_SOURCES)
             square_tile(0)
+            if 0 <= subtracted < PAIRS:
+                lift(subtracted, SOURCES - 2)
+            square_tile(1)
             if 0 <= turned < PAIRS:
                 turn(2 * turned)
                 hand_over(2 * turned)
-            square_tile(1)
-            if 0 <= turned < PAIRS:
                 turn(2 * turned + 1)
                 widen(turned)
             if tick == TURN_AT:
-                spread_centre()
+                spread_centres()
             square_tile(2)
             if 0 <= subtracted < PAIRS:
                 make(subtracted)
             square_tile(3)
             if 0 <= subtracted < PAIRS:
-                lift(subtracted)
+                lift(subtracted, SOURCES - 1)
             if tick == EARLY_AT:
                 roots(early)
 
-            if 0 <= subtracted < PAIRS:
-                subtract(2 * subtracted, slice(0, HELPED_FROM), SOURCES)
-                subtract(2 * subtracted + 1, slice(MADE, LIFTED_TILE * P), SOURCES)
-                subtract(2 * subtracted + 1, slice(LIFTED_TILE * P, GROUP), LIFTED_SOURCE)
             if 0 <= quantised < PAIRS:
                 quantise(2 * quantised)
                 quantise(2 * quantised + 1)

@@ -334,9 +334,9 @@ def tile_moe_pa_t_e_kernel(tc, encodings, domain_encs, Us_words, Us_scales, out)
                 subtract(2 * subtracted + 1, slice(MADE, LIFTED_TILE * P), SOURCES)
                 subtract(2 * subtracted + 1, slice(LIFTED_TILE * P, GROUP), WHOLE_SOURCES)
             square_tile(0)
+            square_tile(1)
             if 0 <= subtracted < PAIRS:
                 lift(subtracted, SOURCES - 2)
-            square_tile(1)
             if 0 <= turned < PAIRS:
                 turn(2 * turned)
                 hand_over(2 * turned)
@@ -345,10 +345,9 @@ def tile_moe_pa_t_e_kernel(tc, encodings, domain_encs, Us_words, Us_scales, out)
             if tick == TURN_AT:
                 spread_centres()
             square_tile(2)
-            if 0 <= subtracted < PAIRS:
-                make(subtracted)
             square_tile(3)
             if 0 <= subtracted < PAIRS:
+                make(subtracted)
                 lift(subtracted, SOURCES - 1)
             if tick == EARLY_AT:
                 roots(early)

@@ -31,7 +31,9 @@ WORDS = HIDDEN // 2
 HELPED = 72
 HELPED_FROM = GROUP - HELPED
 MADE = 51
-MADE_ROWS = 64
+MADE_ROWS = 52
+COPIES = 2
+COPY_ROWS = P // COPIES
 MADE_TILES = 3
 LIFTED_SOURCES = 2
 WHOLE_SOURCES = SOURCES - LIFTED_SOURCES
@@ -80,10 +82,11 @@ def tile_moe_pa_t_e_kernel(tc, encodings, domain_encs, Us_words, Us_scales, out)
             enc_of[g] = enc_sb
 
         def load_made(q):
-            nc.sync.dma_start(
-                out=made_rows[q % MADE_TILES][:MADE_ROWS, :],
-                in_=enc_rows[:MADE_ROWS, q * PAIR_TILES + GROUP_TILES, :],
-            )
+            for b in range(COPIES):
+                nc.sync.dma_start(
+                    out=made_rows[q % MADE_TILES][b * COPY_ROWS : b * COPY_ROWS + MADE_ROWS, : HIDDEN - b],
+                    in_=enc_rows[:MADE_ROWS, q * PAIR_TILES + GROUP_TILES, b:],
+                )
 
         def turn(g):
             planes = plane_pool.tile([P, GROUP, HALVES], F32)
@@ -107,18 +110,18 @@ def tile_moe_pa_t_e_kernel(tc, encodings, domain_encs, Us_words, Us_scales, out)
             turned_of[g] = turned
 
         def make(q):
-            made = made_pool.tile([P, PACK, SOURCES * MADE], BF16)
-            for t in range(PACK):
+            made = made_pool.tile([P, SOURCES * MADE, PACK], BF16)
+            for t in range(0, PACK, COPIES):
                 nc.tensor.matmul(
-                    out=made[:, t, :],
+                    out=made[:, :, t : t + COPIES],
                     lhsT=made_rows[q % MADE_TILES][:, t:HIDDEN:PACK],
-                    rhs=chooser[:].rearrange("p s n -> p (s n)"),
+                    rhs=chooser[:].rearrange("p s n b -> p (s n) b"),
                     start=True,
                     stop=True,
                 )
             nc.scalar.copy(
                 out=diff_of[2 * q + 1][:, :, :MADE, :],
-                in_=made[:].rearrange("p t (s n) -> p s n t", s=SOURCES),
+                in_=made[:].rearrange("p (s n) t -> p s n t", s=SOURCES),
             )
 
         def widen(q):
@@ -215,17 +218,21 @@ def tile_moe_pa_t_e_kernel(tc, encodings, domain_encs, Us_words, Us_scales, out)
         for i in range(MADE_TILES):
             rows = const.tile([P, HIDDEN], BF16, name="made_rows%d" % i)
             nc.vector.memset(rows[:].bitcast(I32), 0)
-            nc.scalar.dma_start(out=rows[MADE_ROWS : MADE_ROWS + SOURCES, :], in_=domain_encs)
+            for b in range(COPIES):
+                centres = slice(b * COPY_ROWS + MADE_ROWS, b * COPY_ROWS + MADE_ROWS + SOURCES)
+                nc.scalar.dma_start(out=rows[centres, : HIDDEN - b], in_=domain_encs[:, b:])
             made_rows.append(rows)
-        chooser = const.tile([P, SOURCES, MADE], BF16)
-        nc.gpsimd.tensor_tensor(
-            out=chooser[:],
-            in0=identity_bf[:, :MADE].unsqueeze(1).to_broadcast([P, SOURCES, MADE]),
-            in1=identity_bf[:, MADE_ROWS : MADE_ROWS + SOURCES]
-            .unsqueeze(2)
-            .to_broadcast([P, SOURCES, MADE]),
-            op=ALU.subtract,
-        )
+        chooser = const.tile([P, SOURCES, MADE, COPIES], BF16)
+        for b in range(COPIES):
+            mine = identity_bf[:, b * COPY_ROWS : (b + 1) * COPY_ROWS]
+            nc.gpsimd.tensor_tensor(
+                out=chooser[:, :, :, b],
+                in0=mine[:, :MADE].unsqueeze(1).to_broadcast([P, SOURCES, MADE]),
+                in1=mine[:, MADE_ROWS : MADE_ROWS + SOURCES]
+                .unsqueeze(2)
+                .to_broadcast([P, SOURCES, MADE]),
+                op=ALU.subtract,
+            )
         neg_dom = const.tile([P, SOURCES, PACK], F32)
         neg_centre = {}
 

@@ -37,13 +37,14 @@ COPY_ROWS = P // COPIES
 MADE_TILES = 3
 LIFTED_SOURCES = 2
 WHOLE_SOURCES = SOURCES - LIFTED_SOURCES
+LIFTED_PAIRS = PAIRS - 1
 LIFTED_TILE = GROUP_TILES - 1
 
 FLOPS = 2 * SOURCES * TOKENS * HIDDEN * RANK
 
 SQRT_FLOOR = 2.0 ** -116
 
-LATE_PAIRS = 2
+LATE_PAIRS = 3
 EARLY_TILES = TILES - LATE_PAIRS * PAIR_TILES
 
 LOAD_AT = 0
@@ -210,6 +211,9 @@ def tile_moe_pa_t_e_kernel(tc, encodings, domain_encs, Us_words, Us_scales, out)
 
         dom_t = const.tile([P, SOURCES, PACK], BF16)
         nc.scalar.dma_start(out=dom_t[:], in_=domain_encs.rearrange("s (p t) -> p s t", t=PACK))
+        warm = const.tile([P, 1], F32)
+        nc.vector.memset(warm[:], 1.0)
+        nc.scalar.activation(out=warm[:], in_=warm[:], func=ACT.Sqrt)
         identity = const.tile([P, P], F32)
         make_identity(nc, identity[:])
         identity_bf = const.tile([P, P], BF16)
@@ -218,10 +222,16 @@ def tile_moe_pa_t_e_kernel(tc, encodings, domain_encs, Us_words, Us_scales, out)
         for i in range(MADE_TILES):
             rows = const.tile([P, HIDDEN], BF16, name="made_rows%d" % i)
             nc.vector.memset(rows[:].bitcast(I32), 0)
-            for b in range(COPIES):
-                centres = slice(b * COPY_ROWS + MADE_ROWS, b * COPY_ROWS + MADE_ROWS + SOURCES)
-                nc.scalar.dma_start(out=rows[centres, : HIDDEN - b], in_=domain_encs[:, b:])
             made_rows.append(rows)
+
+        def load_centres():
+            for rows in made_rows:
+                for b in range(COPIES):
+                    first = b * COPY_ROWS + MADE_ROWS
+                    nc.sync.dma_start(
+                        out=rows[first : first + SOURCES, : HIDDEN - b], in_=domain_encs[:, b:]
+                    )
+
         chooser = const.tile([P, SOURCES, MADE, COPIES], BF16)
         for b in range(COPIES):
             mine = identity_bf[:, b * COPY_ROWS : (b + 1) * COPY_ROWS]
@@ -248,9 +258,6 @@ def tile_moe_pa_t_e_kernel(tc, encodings, domain_encs, Us_words, Us_scales, out)
                 nc.scalar.copy(out=centre[:], in_=lifted[:])
                 neg_centre[s] = centre
 
-        warm = const.tile([P, 1], F32)
-        nc.vector.memset(warm[:], 1.0)
-        nc.scalar.activation(out=warm[:], in_=warm[:], func=ACT.Sqrt)
         dist_sq = const.tile([P, SOURCES, TILES], F32)
         u_words = const.tile([P, SOURCES, 2 * RANK], U8, align_bytes=64)
         u_scales = const.tile([P, SOURCES, RANK], U8, align_bytes=64)
@@ -327,6 +334,8 @@ def tile_moe_pa_t_e_kernel(tc, encodings, domain_encs, Us_words, Us_scales, out)
             if 0 <= loaded < PAIRS:
                 load(2 * loaded)
                 load(2 * loaded + 1)
+            if tick == TURN_AT - 1:
+                load_centres()
             if 0 <= turned < PAIRS:
                 load_made(turned)
             if tick == TURN_AT:
@@ -338,16 +347,20 @@ def tile_moe_pa_t_e_kernel(tc, encodings, domain_encs, Us_words, Us_scales, out)
 
             if 0 <= subtracted < PAIRS:
                 subtract(2 * subtracted, slice(0, HELPED_FROM), SOURCES)
-                subtract(2 * subtracted + 1, slice(MADE, LIFTED_TILE * P), SOURCES)
-                subtract(2 * subtracted + 1, slice(LIFTED_TILE * P, GROUP), WHOLE_SOURCES)
+                if subtracted < LIFTED_PAIRS:
+                    subtract(2 * subtracted + 1, slice(MADE, LIFTED_TILE * P), SOURCES)
+                    subtract(2 * subtracted + 1, slice(LIFTED_TILE * P, GROUP), WHOLE_SOURCES)
+                else:
+                    subtract(2 * subtracted + 1, slice(MADE, GROUP), SOURCES)
             square_tile(0)
             square_tile(1)
-            if 0 <= subtracted < PAIRS:
+            if 0 <= subtracted < LIFTED_PAIRS:
                 lift(subtracted, SOURCES - 2)
             if 0 <= turned < PAIRS:
                 turn(2 * turned)
                 hand_over(2 * turned)
                 turn(2 * turned + 1)
+            if 0 <= turned < LIFTED_PAIRS:
                 widen(turned)
             if tick == TURN_AT:
                 spread_centres()
@@ -355,6 +368,7 @@ def tile_moe_pa_t_e_kernel(tc, encodings, domain_encs, Us_words, Us_scales, out)
             square_tile(3)
             if 0 <= subtracted < PAIRS:
                 make(subtracted)
+            if 0 <= subtracted < LIFTED_PAIRS:
                 lift(subtracted, SOURCES - 1)
             if tick == EARLY_AT:
                 roots(early)

@@ -28,9 +28,9 @@ PAIRS = TILES // PAIR_TILES
 HALVES = 2
 WORDS = HIDDEN // 2
 
-HELPED = 72
+HELPED = 76
 HELPED_FROM = GROUP - HELPED
-MADE = 51
+MADE = 50
 MADE_ROWS = 52
 COPIES = 2
 COPY_ROWS = P // COPIES

from contextlib import ExitStack

import concourse.mybir as mybir
from concourse.masks import make_identity

F32 = mybir.dt.float32
BF16 = mybir.dt.bfloat16
I32 = mybir.dt.int32
U32 = mybir.dt.uint32
U8 = mybir.dt.uint8
FP8X4 = mybir.dt.float8_e4m3fn_x4
FP4X4 = mybir.dt.float4_e2m1fn_x4
ALU = mybir.AluOpType
ACT = mybir.ActivationFunctionType
AXIS_X = mybir.AxisListType.X

P = 128
PACK = 4
TOKENS, HIDDEN, SOURCES, RANK = 16384, 512, 4, 128
assert HIDDEN == P * PACK

TILES = TOKENS // P
GROUP_TILES = 2
GROUP = GROUP_TILES * P
PAIR_GROUPS = 2
PAIR_TILES = PAIR_GROUPS * GROUP_TILES
PAIRS = TILES // PAIR_TILES
HALVES = 2
WORDS = HIDDEN // 2

HELPED = 76
HELPED_FROM = GROUP - HELPED
MADE = 50
MADE_ROWS = 52
COPIES = 2
COPY_ROWS = P // COPIES
MADE_TILES = 3
LIFTED_SOURCES = 2
WHOLE_SOURCES = SOURCES - LIFTED_SOURCES
LIFTED_PAIRS = PAIRS - 1
LIFTED_TILE = GROUP_TILES - 1

FLOPS = 2 * SOURCES * TOKENS * HIDDEN * RANK

SQRT_FLOOR = 2.0 ** -116

LATE_PAIRS = 3
EARLY_TILES = TILES - LATE_PAIRS * PAIR_TILES

LOAD_AT = 0
TURN_AT = 2
SUBTRACT_AT = TURN_AT + 1
QUANTISE_AT = SUBTRACT_AT + 1
PROJECT_AT = QUANTISE_AT + 1
EARLY_AT = PAIRS - LATE_PAIRS - 1 + PROJECT_AT + 1


def tile_moe_pa_t_e_kernel(tc, encodings, domain_encs, Us_words, Us_scales, out):
    nc = tc.nc
    enc_rows = encodings.rearrange("(i j) k -> i j k", j=TILES)
    out_cols = out.rearrange("s (i j) -> i s j", j=TILES)

    with ExitStack() as ctx:
        ctx.enter_context(tc.manual_schedule())
        const = ctx.enter_context(tc.tile_pool(name="const", bufs=1))
        enc_pool = ctx.enter_context(tc.tile_pool(name="enc", bufs=2 * (TURN_AT + 2)))
        turned_pool = ctx.enter_context(tc.tile_pool(name="turned", bufs=2))
        diff_pool = ctx.enter_context(tc.tile_pool(name="diff", bufs=2))
        code_pool = ctx.enter_context(tc.tile_pool(name="code", bufs=6))
        square_pool = ctx.enter_context(tc.tile_pool(name="square", bufs=2))
        plane_pool = ctx.enter_context(tc.psum_pool(name="plane", bufs=3))
        proj_pool = ctx.enter_context(tc.psum_pool(name="proj", bufs=2))
        made_pool = ctx.enter_context(tc.psum_pool(name="made", bufs=1))
        lifted_pool = ctx.enter_context(tc.psum_pool(name="lifted", bufs=2))
        wide_pool = ctx.enter_context(tc.tile_pool(name="wide", bufs=2))

        enc_of, planes_of, turned_of, diff_of, codes_of, scales_of, wide_of = {}, {}, {}, {}, {}, {}, {}

        def load(g):
            enc_sb = enc_pool.tile([P, GROUP_TILES, HIDDEN], BF16)
            first = g * GROUP_TILES
            nc.sync.dma_start(out=enc_sb[:], in_=enc_rows[:, first : first + GROUP_TILES, :])
            enc_of[g] = enc_sb

        def load_made(q):
            for b in range(COPIES):
                nc.sync.dma_start(
                    out=made_rows[q % MADE_TILES][b * COPY_ROWS : b * COPY_ROWS + MADE_ROWS, : HIDDEN - b],
                    in_=enc_rows[:MADE_ROWS, q * PAIR_TILES + GROUP_TILES, b:],
                )

        def turn(g):
            planes = plane_pool.tile([P, GROUP, HALVES], F32)
            for h in range(GROUP_TILES):
                words = enc_of[g][:, h, :].bitcast(F32)
                for u in range(HALVES):
                    nc.tensor.transpose(
                        planes[:, h * P : (h + 1) * P, u], words[:, u:WORDS:HALVES], identity[:]
                    )
            planes_of[g] = planes

        def hand_over(g):
            turned = turned_pool.tile([P, HELPED, PACK], BF16)
            nc.scalar.copy(
                out=turned[:]
                .rearrange("p n t -> p (n t)")
                .bitcast(F32)
                .rearrange("p (n u) -> p n u", u=HALVES),
                in_=planes_of[g][:, HELPED_FROM:, :],
            )
            turned_of[g] = turned

        def make(q):
            made = made_pool.tile([P, SOURCES * MADE, PACK], BF16)
            for t in range(0, PACK, COPIES):
                nc.tensor.matmul(
                    out=made[:, :, t : t + COPIES],
                    lhsT=made_rows[q % MADE_TILES][:, t:HIDDEN:PACK],
                    rhs=chooser[:].rearrange("p s n b -> p (s n) b"),
                    start=True,
                    stop=True,
                )
            nc.scalar.copy(
                out=diff_of[2 * q + 1][:, :, :MADE, :],
                in_=made[:].rearrange("p (s n) t -> p s n t", s=SOURCES),
            )

        def widen(q):
            wide = wide_pool.tile([P, PACK, P], F32)
            nc.scalar.copy(
                out=wide[:],
                in_=enc_of[2 * q + 1][:, LIFTED_TILE, :].rearrange("n (p t) -> n t p", t=PACK),
            )
            wide_of[q] = wide

        def lift(q, s):
            lifted = lifted_pool.tile([P, PACK, P], F32)
            for source, first in ((neg_centre[s], True), (wide_of[q], False)):
                for t in range(PACK):
                    nc.tensor.matmul(
                        out=lifted[:, t, :],
                        lhsT=source[:, t, :],
                        rhs=identity[:],
                        is_transpose=True,
                        start=first and t == 0,
                        stop=not first and t == PACK - 1,
                    )
            nc.scalar.copy(
                out=diff_of[2 * q + 1][:, s, LIFTED_TILE * P :, :],
                in_=lifted[:].rearrange("p t n -> p n t"),
            )

        def open_diff(q):
            first = diff_pool.tile([P, SOURCES, GROUP, PACK], BF16, align_bytes=64)
            second = diff_pool.tile([P, SOURCES, GROUP, PACK], BF16, align_bytes=64)
            diff_of[2 * q], diff_of[2 * q + 1] = first, second

        def help_subtract(g):
            shape = [P, SOURCES, HELPED, PACK]
            nc.gpsimd.tensor_tensor(
                out=diff_of[g][:, :, HELPED_FROM:, :],
                in0=turned_of[g][:].unsqueeze(1).to_broadcast(shape),
                in1=dom_t[:].unsqueeze(2).to_broadcast(shape),
                op=ALU.subtract,
            )

        def subtract(g, tokens, sources):
            values = planes_of[g][:].rearrange("p n u -> p (n u)").bitcast(BF16)
            shape = [P, sources, tokens.stop - tokens.start, PACK]
            nc.vector.tensor_tensor(
                out=diff_of[g][:, :sources, tokens, :],
                in0=values.rearrange("p (n t) -> p n t", t=PACK)[:, tokens, :]
                .unsqueeze(1)
                .to_broadcast(shape),
                in1=dom_t[:, :sources, :].unsqueeze(2).to_broadcast(shape),
                op=ALU.subtract,
            )

        def quantise(g):
            codes = code_pool.tile([P, SOURCES, GROUP], U32, align_bytes=64)
            scales = code_pool.tile([P, SOURCES, GROUP], U8, align_bytes=64)
            nc.vector.quantize_mx(
                out=codes[:].rearrange("p s n -> p (s n)").bitcast(FP8X4),
                scales=scales[:].rearrange("p s n -> p (s n)"),
                in_=diff_of[g][:].rearrange("p s n t -> p (s n t)"),
            )
            codes_of[g], scales_of[g] = codes, scales

        def project(j):
            g, h = j // GROUP_TILES, j % GROUP_TILES
            squares = square_pool.tile([P, SOURCES, RANK], F32)
            proj = proj_pool.tile([P, SOURCES, RANK], F32)
            tokens = slice(h * P, (h + 1) * P)
            for s in range(SOURCES):
                nc.tensor.matmul_mx(
                    out=proj[:, s, :],
                    lhsT=codes_of[g][:, s, tokens].bitcast(FP8X4),
                    lhsT_scale=scales_of[g][:, s, tokens],
                    rhs=u_words[:, s, :].bitcast(FP4X4),
                    rhs_scale=u_scales[:, s, :],
                    start=True,
                    stop=True,
                )
            for s in range(SOURCES):
                nc.scalar.activation(
                    out=squares[:, s, :],
                    in_=proj[:, s, :],
                    func=ACT.Square,
                    accum_out=dist_sq[:, s, j : j + 1],
                )

        dom_t = const.tile([P, SOURCES, PACK], BF16)
        nc.scalar.dma_start(out=dom_t[:], in_=domain_encs.rearrange("s (p t) -> p s t", t=PACK))
        warm = const.tile([P, 1], F32)
        nc.vector.memset(warm[:], 1.0)
        nc.scalar.activation(out=warm[:], in_=warm[:], func=ACT.Sqrt)
        identity = const.tile([P, P], F32)
        make_identity(nc, identity[:])
        identity_bf = const.tile([P, P], BF16)
        make_identity(nc, identity_bf[:])
        made_rows = []
        for i in range(MADE_TILES):
            rows = const.tile([P, HIDDEN], BF16, name="made_rows%d" % i)
            nc.vector.memset(rows[:].bitcast(I32), 0)
            made_rows.append(rows)

        def load_centres():
            for rows in made_rows:
                for b in range(COPIES):
                    first = b * COPY_ROWS + MADE_ROWS
                    nc.sync.dma_start(
                        out=rows[first : first + SOURCES, : HIDDEN - b], in_=domain_encs[:, b:]
                    )

        chooser = const.tile([P, SOURCES, MADE, COPIES], BF16)
        for b in range(COPIES):
            mine = identity_bf[:, b * COPY_ROWS : (b + 1) * COPY_ROWS]
            nc.gpsimd.tensor_tensor(
                out=chooser[:, :, :, b],
                in0=mine[:, :MADE].unsqueeze(1).to_broadcast([P, SOURCES, MADE]),
                in1=mine[:, MADE_ROWS : MADE_ROWS + SOURCES]
                .unsqueeze(2)
                .to_broadcast([P, SOURCES, MADE]),
                op=ALU.subtract,
            )
        neg_dom = const.tile([P, SOURCES, PACK], F32)
        neg_centre = {}

        def spread_centres():
            nc.vector.tensor_scalar_mul(out=neg_dom[:], in0=dom_t[:], scalar1=-1.0)
            for s in range(WHOLE_SOURCES, SOURCES):
                lifted = lifted_pool.tile([P, PACK, P], F32)
                for t in range(PACK):
                    nc.tensor.transpose(
                        lifted[:, t, :], neg_dom[:, s, t : t + 1].to_broadcast([P, P]), identity[:]
                    )
                centre = const.tile([P, PACK, P], F32, name="centre%d" % s)
                nc.scalar.copy(out=centre[:], in_=lifted[:])
                neg_centre[s] = centre

        dist_sq = const.tile([P, SOURCES, TILES], F32)
        u_words = const.tile([P, SOURCES, 2 * RANK], U8, align_bytes=64)
        u_scales = const.tile([P, SOURCES, RANK], U8, align_bytes=64)
        nc.vector.memset(u_scales[:].bitcast(I32), 0)

        def load_weights():
            nc.sync.dma_start(
                out=u_words[:].bitcast(I32), in_=Us_words.rearrange("s p b -> p s b").bitcast(I32)
            )
            for quadrant in range(4):
                nc.sync.dma_start(
                    out=u_scales[32 * quadrant : 32 * quadrant + 4].bitcast(I32),
                    in_=Us_scales[:, 4 * quadrant : 4 * quadrant + 4, :]
                    .rearrange("s r n -> r s n")
                    .bitcast(I32),
                )

        dist = const.tile([P, SOURCES, TILES], F32)
        nearest = const.tile([P, TILES], F32)
        weight = const.tile([P, SOURCES, TILES], F32)
        total = const.tile([P, TILES], F32)
        floor = const.tile([P, 1], F32)
        nc.vector.memset(floor[:], SQRT_FLOOR)

        def roots(tiles):
            nc.scalar.activation(
                out=dist[:, :, tiles], in_=dist_sq[:, :, tiles], func=ACT.Sqrt, bias=floor[:]
            )

        def shift(tiles):
            count = tiles.stop - tiles.start
            nc.vector.tensor_reduce(
                out=nearest[:, tiles],
                in_=dist[:, :, tiles].rearrange("p s j -> p j s"),
                axis=AXIS_X,
                op=ALU.min,
            )
            nc.vector.tensor_tensor(
                out=dist[:, :, tiles],
                in0=dist[:, :, tiles],
                in1=nearest[:, tiles].unsqueeze(1).to_broadcast([P, SOURCES, count]),
                op=ALU.subtract,
            )

        def weigh(tiles):
            nc.scalar.activation(out=weight[:, :, tiles], in_=dist[:, :, tiles], func=ACT.Exp, scale=-1.0)

        def share(tiles):
            count = tiles.stop - tiles.start
            nc.vector.tensor_reduce(
                out=total[:, tiles],
                in_=weight[:, :, tiles].rearrange("p s j -> p j s"),
                axis=AXIS_X,
                op=ALU.add,
            )
            nc.vector.reciprocal(out=total[:, tiles], in_=total[:, tiles])
            nc.vector.tensor_tensor(
                out=weight[:, :, tiles],
                in0=weight[:, :, tiles],
                in1=total[:, tiles].unsqueeze(1).to_broadcast([P, SOURCES, count]),
                op=ALU.mult,
            )
            nc.sync.dma_start(out=out_cols[:, :, tiles], in_=weight[:, :, tiles])

        early = slice(0, EARLY_TILES)
        late = slice(EARLY_TILES, TILES)

        for tick in range(PAIRS + PROJECT_AT):
            loaded = tick - LOAD_AT
            turned = tick - TURN_AT
            subtracted = tick - SUBTRACT_AT
            quantised = tick - QUANTISE_AT
            projected = tick - PROJECT_AT
            if 0 <= loaded < PAIRS:
                load(2 * loaded)
                load(2 * loaded + 1)
            if tick == TURN_AT - 1:
                load_centres()
            if 0 <= turned < PAIRS:
                load_made(turned)
            if tick == TURN_AT:
                load_weights()

            def square_tile(i):
                if 0 <= projected < PAIRS:
                    project(projected * PAIR_TILES + i)

            if 0 <= subtracted < PAIRS:
                subtract(2 * subtracted, slice(0, HELPED_FROM), SOURCES)
                if subtracted < LIFTED_PAIRS:
                    subtract(2 * subtracted + 1, slice(MADE, LIFTED_TILE * P), SOURCES)
                    subtract(2 * subtracted + 1, slice(LIFTED_TILE * P, GROUP), WHOLE_SOURCES)
                else:
                    subtract(2 * subtracted + 1, slice(MADE, GROUP), SOURCES)
            square_tile(0)
            square_tile(1)
            if 0 <= subtracted < LIFTED_PAIRS:
                lift(subtracted, SOURCES - 2)
            if 0 <= turned < PAIRS:
                turn(2 * turned)
                hand_over(2 * turned)
                turn(2 * turned + 1)
            if 0 <= turned < LIFTED_PAIRS:
                widen(turned)
            if tick == TURN_AT:
                spread_centres()
            square_tile(2)
            square_tile(3)
            if 0 <= subtracted < PAIRS:
                make(subtracted)
            if 0 <= subtracted < LIFTED_PAIRS:
                lift(subtracted, SOURCES - 1)
            if tick == EARLY_AT:
                roots(early)

            if 0 <= quantised < PAIRS:
                quantise(2 * quantised)
                quantise(2 * quantised + 1)
            if 0 <= turned < PAIRS:
                open_diff(turned)
                help_subtract(2 * turned)

        shift(early)
        roots(late)
        shift(late)
        weigh(slice(0, TILES))
        share(slice(0, TILES))
